import numpy as np
import ml_dtypes


def mxq(x, axis, fmt="e4m3"):
    dtype, down = {"e4m3": (ml_dtypes.float8_e4m3fn, 7), "e5m2": (ml_dtypes.float8_e5m2, 14)}[fmt]
    v = np.moveaxis(np.asarray(x, np.float32).astype(ml_dtypes.bfloat16).astype(np.float64), axis, -1)
    blocks = v.reshape(v.shape[:-1] + (-1, 32))
    amax = np.abs(blocks).max(-1, keepdims=True)
    byte = np.maximum(np.where(amax > 0, np.frexp(amax)[1] - 1 + 127, 0) - down, 1)
    scale = np.exp2(byte - 127.0)
    codes = (blocks / scale).astype(np.float32).astype(dtype).astype(np.float64)
    return np.moveaxis((codes * scale).reshape(v.shape), -1, axis)


WIDE = False


def mx_kscale(k):
    if not WIDE:
        return np.ones(k)
    levels = np.array([30, -30])
    if k % 512:
        return np.exp2(np.random.permutation(np.resize(levels, k // 32))).repeat(32)
    a = np.empty((k // 512, 16))
    for p in range(k // 512):
        a[p, :8] = np.random.permutation(np.resize(levels, 8))
        for g in range(8):
            far = levels[np.abs(levels - a[p, g]) >= 10]
            a[p, g + 8] = far[np.random.randint(len(far))]
    return np.exp2(a.ravel()).repeat(32)


BF16 = ml_dtypes.bfloat16


def bf(x):
    return np.asarray(x, np.float32).astype(BF16)


def f64(x):
    return np.asarray(x).astype(np.float64)


B, S, D, H = 1, 512, 2048, 16
HD = D // H
HALF = HD // 2


def rotary(v, cos, sin):
    p = v.reshape(B, S, H, HALF, 2)
    vr, vi = p[..., 0], p[..., 1]
    c = cos[None, :, None, :]
    s = sin[None, :, None, :]
    return np.stack([vr * c - vi * s, vr * s + vi * c], axis=-1).reshape(B, S, H, HD)


def setup_inputs():
    s = mx_kscale(D)
    inv_freq = 1.0 / (10000.0 ** (np.arange(0, HD, 2) / HD))
    angles = np.arange(S)[:, None] * inv_freq[None, :]
    return {"x": bf(np.random.standard_normal((B, S, D)) * s),
            "freqs_cos": bf(np.cos(angles)), "freqs_sin": bf(np.sin(angles)),
            "wq": bf(np.random.standard_normal((D, D)) * 1.4 / np.sqrt(D) / s[:, None]),
            "wk": bf(np.random.standard_normal((D, D)) * 1.4 / np.sqrt(D) / s[:, None])}


def reference(x, freqs_cos, freqs_sin, wq, wk):
    xq = mxq(f64(x), 2, "e5m2")
    q = (xq @ mxq(f64(wq), 0, "e5m2")).reshape(B, S, H, HD)
    k = (xq @ mxq(f64(wk), 0, "e5m2")).reshape(B, S, H, HD)
    c, s = f64(freqs_cos), f64(freqs_sin)
    return rotary(q, c, s), rotary(k, c, s)

@@ -1,0 +1,226 @@
+from contextlib import ExitStack
+
+import concourse.mybir as mybir
+from concourse.masks import make_identity
+
+F32 = mybir.dt.float32
+BF16 = mybir.dt.bfloat16
+U32 = mybir.dt.uint32
+U8 = mybir.dt.uint8
+E5X4 = mybir.dt.float8_e5m2_x4
+MULT = mybir.AluOpType.mult
+ADD = mybir.AluOpType.add
+
+P = 128
+TOK = 512
+K = 2048
+NF = 2048
+PACK = 4
+KP = P * PACK
+PASSES = K // KP
+MT = TOK // P
+NB = 512
+UNITS = 2 * NF // NB
+TILES = UNITS * PASSES
+FLOPS = 2 * TOK * K * 2 * NF
+
+V_TILES = ()
+G_ADD_M = ()
+MANUAL = True
+
+
+def tile_attention_pa_kernel(tc, x, freqs_cos, freqs_sin, wq, wk, out_0, out_1):
+    nc = tc.nc
+    x2 = x.rearrange("b s k -> (b s) k")
+    outs = [out_0.rearrange("b s h d -> (b s) (h d)"), out_1.rearrange("b s h d -> (b s) (h d)")]
+    ws = [wq, wk]
+
+    with ExitStack() as ctx:
+        const = ctx.enter_context(tc.tile_pool(name="const", bufs=1))
+        xpool = ctx.enter_context(tc.tile_pool(name="xpool", bufs=4))
+        xgpool = ctx.enter_context(tc.tile_pool(name="xgpool", bufs=2))
+        rawh_pool = ctx.enter_context(tc.tile_pool(name="rawh", bufs=8))
+        raw_pool = ctx.enter_context(tc.tile_pool(name="raw", bufs=8))
+        gpool = ctx.enter_context(tc.tile_pool(name="grp", bufs=4))
+        cpool = ctx.enter_context(tc.tile_pool(name="codes", bufs=3))
+        rpool = ctx.enter_context(tc.tile_pool(name="prod", bufs=4))
+        opool = ctx.enter_context(tc.tile_pool(name="outp", bufs=6))
+        psum = ctx.enter_context(tc.psum_pool(name="psum", bufs=8))
+        if MANUAL:
+            ctx.enter_context(tc.manual_schedule())
+
+        ident = const.tile([P, P], F32)
+        make_identity(nc, ident[:])
+        warm_in = const.tile([P, 8], F32)
+        warm_out = const.tile([P, 8], F32)
+        nc.vector.memset(warm_in[:], 0.0)
+        nc.scalar.copy(out=warm_out[:], in_=warm_in[:])
+
+        cos_raw = const.tile([P, MT, 64], BF16)
+        sin_raw = const.tile([P, MT, 64], BF16)
+        tab = const.tile([P, MT, 2, P], F32)
+        x_codes = const.tile([P, MT, KP], U32, align_bytes=64)
+        x_scales = const.tile([P, MT, KP], U8, align_bytes=64)
+
+        raw = {}
+        x_sb = {}
+        xt = {}
+        xg = {}
+        grouped = {}
+        w_codes = {}
+        w_scales = {}
+        acc = {}
+        prod = {}
+
+        def load_x(m):
+            t = xpool.tile([P, K], BF16, tag="x_sb")
+            nc.sync.dma_start(out=t[:], in_=x2[m * P : (m + 1) * P, :])
+            x_sb[m] = t
+
+        def load_half(u, g):
+            t = rawh_pool.tile([P, PACK, NB], BF16, tag="rawh")
+            w, nb = divmod(u, 4)
+            nc.sync.dma_start(
+                out=t[:],
+                in_=ws[w][g * KP : (g + 1) * KP, nb * NB : (nb + 1) * NB].rearrange("(p j) n -> p j n", j=PACK),
+            )
+            raw[(u, g)] = t[:]
+
+        def load_pair(cp, g):
+            t = raw_pool.tile([P, PACK, 2 * NB], BF16, tag="raw")
+            w, c = divmod(cp, 2)
+            nc.sync.dma_start(
+                out=t[:],
+                in_=ws[w][g * KP : (g + 1) * KP, c * 2 * NB : (c + 1) * 2 * NB].rearrange("(p j) n -> p j n", j=PACK),
+            )
+            raw[(2 * cp, g)] = t[:, :, 0:NB]
+            raw[(2 * cp + 1, g)] = t[:, :, NB : 2 * NB]
+
+        def xpose(m):
+            words = x_sb[m][:].bitcast(F32)
+            for hb in range(2):
+                bank = psum.tile([P, 4, P], F32, tag="bank")
+                for gg in range(2):
+                    g = 2 * hb + gg
+                    for u in range(2):
+                        nc.tensor.transpose(bank[:, 2 * gg + u, :], words[:, 256 * g + u : 256 * (g + 1) : 2], ident[:])
+                xt[(m, hb)] = bank
+
+        def evac(m):
+            t = xgpool.tile([P, K], BF16, tag="xg", align_bytes=64)
+            tw = t[:].bitcast(F32).rearrange("p (g r u) -> p g r u", g=PASSES, u=2)
+            for hb in range(2):
+                nc.vector.tensor_copy(
+                    out=tw[:, 2 * hb : 2 * hb + 2, :, :],
+                    in_=xt[(m, hb)][:].rearrange("p (gg u) r -> p gg r u", u=2),
+                )
+            xg[m] = t
+
+        def xquant(m):
+            nc.vector.quantize_mx(out=x_codes[:, m, :].bitcast(E5X4), scales=x_scales[:, m, :], in_=xg[m][:])
+
+        def inter(t_idx):
+            u, g = divmod(t_idx, PASSES)
+            t = gpool.tile([P, NB, PACK], BF16, tag="grp", align_bytes=64)
+            src = raw[(u, g)].rearrange("p j c -> p c j")
+            if t_idx in V_TILES:
+                nc.vector.tensor_copy(out=t[:], in_=src)
+            else:
+                nc.scalar.copy(out=t[:], in_=src)
+            grouped[t_idx] = t
+
+        def quant(t_idx):
+            u, g = divmod(t_idx, PASSES)
+            if g == 0:
+                wc = cpool.tile([P, PASSES, NB], U32, tag="wc", align_bytes=64)
+                wsc = cpool.tile([P, PASSES, NB], U8, tag="wsc", align_bytes=64)
+                w_codes[u] = wc
+                w_scales[u] = wsc
+            nc.vector.quantize_mx(
+                out=w_codes[u][:, g, :].bitcast(E5X4),
+                scales=w_scales[u][:, g, :],
+                in_=grouped[t_idx][:].rearrange("p c j -> p (c j)"),
+            )
+
+        def one_mm(u, m, g):
+            nc.tensor.matmul_mx(
+                out=acc[(u, m)][:],
+                lhsT=x_codes[:, m, g * P : (g + 1) * P].bitcast(E5X4),
+                lhsT_scale=x_scales[:, m, g * P : (g + 1) * P],
+                rhs=w_codes[u][:, g, :].bitcast(E5X4),
+                rhs_scale=w_scales[u][:, g, :],
+                start=(g == 0),
+                stop=(g == PASSES - 1),
+            )
+
+        def new_acc(u, m):
+            bank = psum.tile([P, NB], F32, tag="bank")
+            acc[(u, m)] = bank
+
+        def rot_mul(b_idx):
+            u, m = divmod(b_idx, MT)
+            t = rpool.tile([P, 2, NB], F32, tag="prod")
+            nc.vector.tensor_tensor(
+                out=t[:].rearrange("p r (h j) -> p r h j", h=4),
+                in0=acc[(u, m)][:].rearrange("p (h j) -> p h j", h=4).unsqueeze(1).to_broadcast([P, 2, 4, P]),
+                in1=tab[:, m, :, :].unsqueeze(2).to_broadcast([P, 2, 4, P]),
+                op=MULT,
+            )
+            prod[b_idx] = t
+
+        def rot_add_store(b_idx):
+            u, m = divmod(b_idx, MT)
+            w, nb = divmod(u, 4)
+            o = opool.tile([P, NB], F32, tag="o")
+            eng = nc.gpsimd if m in G_ADD_M else nc.vector
+            eng.tensor_tensor(
+                out=o[:].rearrange("p (n e) -> p n e", e=2),
+                in0=prod[b_idx][:, 0, :].rearrange("p (n e) -> p n e", e=2),
+                in1=prod[b_idx][:, 1, :].rearrange("p (n e) -> p n e", e=2)[:, :, ::-1],
+                op=ADD,
+            )
+            nc.sync.dma_start(out=outs[w][m * P : (m + 1) * P, nb * NB : (nb + 1) * NB], in_=o[:])
+
+        nc.sync.dma_start(out=cos_raw[:], in_=freqs_cos.rearrange("(m p) i -> p m i", p=P))
+        nc.sync.dma_start(out=sin_raw[:], in_=freqs_sin.rearrange("(m p) i -> p m i", p=P))
+        for g in range(PASSES):
+            load_half(0, g)
+            load_x(g)
+        for g in range(PASSES):
+            load_half(1, g)
+        for cp in (1, 2):
+            for g in range(PASSES):
+                load_pair(cp, g)
+
+        tabv = tab[:].rearrange("p m r (i e) -> p m r i e", e=2)
+        nc.vector.tensor_copy(out=tabv[:, :, 0, :, :], in_=cos_raw[:].unsqueeze(3).to_broadcast([P, MT, 64, 2]))
+        nc.vector.tensor_copy(out=tabv[:, :, 1, :, 0], in_=sin_raw[:])
+        nc.vector.tensor_scalar_mul(out=tabv[:, :, 1, :, 1], in0=sin_raw[:], scalar1=-1.0)
+
+        for k in range(TILES + 7):
+            if 13 <= k < 13 + PASSES:
+                load_pair(3, k - 13)
+            if k < MT:
+                xpose(k)
+                evac(k)
+            if k < TILES:
+                inter(k)
+            if 1 <= k <= TILES:
+                quant(k - 1)
+            if k < MT:
+                xquant(k)
+            if k == PASSES:
+                for m in range(MT):
+                    new_acc(0, m)
+                    for g in range(PASSES):
+                        one_mm(0, m, g)
+            elif PASSES < k <= TILES:
+                u, g = divmod(k - 1, PASSES)
+                for m in range(MT):
+                    if g == 0:
+                        new_acc(u, m)
+                    one_mm(u, m, g)
+            if 0 <= k - 5 < TILES:
+                rot_mul(k - 5)
+            if 0 <= k - 6 < TILES:
+                rot_add_store(k - 6)

@@ -21,12 +21,9 @@ PASSES = K // KP
 MT = TOK // P
 NB = 512
 UNITS = 2 * NF // NB
-TILES = UNITS * PASSES
 FLOPS = 2 * TOK * K * 2 * NF
 
-V_TILES = ()
-G_ADD_M = ()
-MANUAL = True
+VCOLS = (0, 512, 320, 320, 320, 320, 320, 320)
 
 
 def tile_attention_pa_kernel(tc, x, freqs_cos, freqs_sin, wq, wk, out_0, out_1):
@@ -42,12 +39,11 @@ def tile_attention_pa_kernel(tc, x, freqs_cos, freqs_sin, wq, wk, out_0, out_1):
         rawh_pool = ctx.enter_context(tc.tile_pool(name="rawh", bufs=8))
         raw_pool = ctx.enter_context(tc.tile_pool(name="raw", bufs=8))
         gpool = ctx.enter_context(tc.tile_pool(name="grp", bufs=4))
-        cpool = ctx.enter_context(tc.tile_pool(name="codes", bufs=3))
+        cpool = ctx.enter_context(tc.tile_pool(name="codes", bufs=2))
         rpool = ctx.enter_context(tc.tile_pool(name="prod", bufs=4))
         opool = ctx.enter_context(tc.tile_pool(name="outp", bufs=6))
         psum = ctx.enter_context(tc.psum_pool(name="psum", bufs=8))
-        if MANUAL:
-            ctx.enter_context(tc.manual_schedule())
+        ctx.enter_context(tc.manual_schedule())
 
         ident = const.tile([P, P], F32)
         make_identity(nc, ident[:])
@@ -119,46 +115,53 @@ def tile_attention_pa_kernel(tc, x, freqs_cos, freqs_sin, wq, wk, out_0, out_1):
         def xquant(m):
             nc.vector.quantize_mx(out=x_codes[:, m, :].bitcast(E5X4), scales=x_scales[:, m, :], in_=xg[m][:])
 
-        def inter(t_idx):
-            u, g = divmod(t_idx, PASSES)
-            t = gpool.tile([P, NB, PACK], BF16, tag="grp", align_bytes=64)
-            src = raw[(u, g)].rearrange("p j c -> p c j")
-            if t_idx in V_TILES:
-                nc.vector.tensor_copy(out=t[:], in_=src)
-            else:
-                nc.scalar.copy(out=t[:], in_=src)
-            grouped[t_idx] = t
+        def inter_scalar(u):
+            for b in range(2):
+                t = gpool.tile([P, 2, NB, PACK], BF16, tag="grp", align_bytes=64)
+                grouped[(u, b)] = t
+                for gg in range(2):
+                    g = 2 * b + gg
+                    cs = NB - VCOLS[u] if g == PASSES - 1 else NB
+                    if cs > 0:
+                        nc.scalar.copy(out=t[:, gg, 0:cs, :], in_=raw[(u, g)][:, :, 0:cs].rearrange("p j c -> p c j"))
 
-        def quant(t_idx):
-            u, g = divmod(t_idx, PASSES)
-            if g == 0:
+        def inter_vector(u):
+            if VCOLS[u] > 0:
+                cs = NB - VCOLS[u]
+                nc.vector.tensor_copy(
+                    out=grouped[(u, 1)][:, 1, cs:NB, :],
+                    in_=raw[(u, PASSES - 1)][:, :, cs:NB].rearrange("p j c -> p c j"),
+                )
+
+        def quant(u, b):
+            if b == 0:
                 wc = cpool.tile([P, PASSES, NB], U32, tag="wc", align_bytes=64)
                 wsc = cpool.tile([P, PASSES, NB], U8, tag="wsc", align_bytes=64)
                 w_codes[u] = wc
                 w_scales[u] = wsc
             nc.vector.quantize_mx(
-                out=w_codes[u][:, g, :].bitcast(E5X4),
-                scales=w_scales[u][:, g, :],
-                in_=grouped[t_idx][:].rearrange("p c j -> p (c j)"),
+                out=w_codes[u][:, 2 * b : 2 * b + 2, :].rearrange("p g c -> p (g c)").bitcast(E5X4),
+                scales=w_scales[u][:, 2 * b : 2 * b + 2, :].rearrange("p g c -> p (g c)"),
+                in_=grouped[(u, b)][:].rearrange("p g c j -> p (g c j)"),
             )
 
-        def one_mm(u, m, g):
-            nc.tensor.matmul_mx(
-                out=acc[(u, m)][:],
-                lhsT=x_codes[:, m, g * P : (g + 1) * P].bitcast(E5X4),
-                lhsT_scale=x_scales[:, m, g * P : (g + 1) * P],
-                rhs=w_codes[u][:, g, :].bitcast(E5X4),
-                rhs_scale=w_scales[u][:, g, :],
-                start=(g == 0),
-                stop=(g == PASSES - 1),
-            )
+        def mm(u, b):
+            for m in range(MT):
+                if b == 0:
+                    bank = psum.tile([P, NB], F32, tag="bank")
+                    acc[(u, m)] = bank
+                for g in (2 * b, 2 * b + 1):
+                    nc.tensor.matmul_mx(
+                        out=acc[(u, m)][:],
+                        lhsT=x_codes[:, m, g * P : (g + 1) * P].bitcast(E5X4),
+                        lhsT_scale=x_scales[:, m, g * P : (g + 1) * P],
+                        rhs=w_codes[u][:, g, :].bitcast(E5X4),
+                        rhs_scale=w_scales[u][:, g, :],
+                        start=(g == 0),
+                        stop=(g == PASSES - 1),
+                    )
 
-        def new_acc(u, m):
-            bank = psum.tile([P, NB], F32, tag="bank")
-            acc[(u, m)] = bank
-
-        def rot_mul(b_idx):
-            u, m = divmod(b_idx, MT)
+        def rot_mul(u, m):
             t = rpool.tile([P, 2, NB], F32, tag="prod")
             nc.vector.tensor_tensor(
                 out=t[:].rearrange("p r (h j) -> p r h j", h=4),
@@ -166,17 +169,15 @@ def tile_attention_pa_kernel(tc, x, freqs_cos, freqs_sin, wq, wk, out_0, out_1):
                 in1=tab[:, m, :, :].unsqueeze(2).to_broadcast([P, 2, 4, P]),
                 op=MULT,
             )
-            prod[b_idx] = t
+            prod[(u, m)] = t
 
-        def rot_add_store(b_idx):
-            u, m = divmod(b_idx, MT)
+        def rot_add_store(eng, u, m):
             w, nb = divmod(u, 4)
             o = opool.tile([P, NB], F32, tag="o")
-            eng = nc.gpsimd if m in G_ADD_M else nc.vector
             eng.tensor_tensor(
                 out=o[:].rearrange("p (n e) -> p n e", e=2),
-                in0=prod[b_idx][:, 0, :].rearrange("p (n e) -> p n e", e=2),
-                in1=prod[b_idx][:, 1, :].rearrange("p (n e) -> p n e", e=2)[:, :, ::-1],
+                in0=prod[(u, m)][:, 0, :].rearrange("p (n e) -> p n e", e=2),
+                in1=prod[(u, m)][:, 1, :].rearrange("p (n e) -> p n e", e=2)[:, :, ::-1],
                 op=ADD,
             )
             nc.sync.dma_start(out=outs[w][m * P : (m + 1) * P, nb * NB : (nb + 1) * NB], in_=o[:])
@@ -197,30 +198,48 @@ def tile_attention_pa_kernel(tc, x, freqs_cos, freqs_sin, wq, wk, out_0, out_1):
         nc.vector.tensor_copy(out=tabv[:, :, 1, :, 0], in_=sin_raw[:])
         nc.vector.tensor_scalar_mul(out=tabv[:, :, 1, :, 1], in0=sin_raw[:], scalar1=-1.0)
 
-        for k in range(TILES + 7):
-            if 13 <= k < 13 + PASSES:
-                load_pair(3, k - 13)
-            if k < MT:
-                xpose(k)
-                evac(k)
-            if k < TILES:
-                inter(k)
-            if 1 <= k <= TILES:
-                quant(k - 1)
-            if k < MT:
-                xquant(k)
-            if k == PASSES:
-                for m in range(MT):
-                    new_acc(0, m)
-                    for g in range(PASSES):
-                        one_mm(0, m, g)
-            elif PASSES < k <= TILES:
-                u, g = divmod(k - 1, PASSES)
-                for m in range(MT):
-                    if g == 0:
-                        new_acc(u, m)
-                    one_mm(u, m, g)
-            if 0 <= k - 5 < TILES:
-                rot_mul(k - 5)
-            if 0 <= k - 6 < TILES:
-                rot_add_store(k - 6)
+        inter_scalar(0)
+        for m in range(MT):
+            xpose(m)
+        evac(0)
+        evac(1)
+        xquant(0)
+        evac(2)
+        xquant(1)
+        quant(0, 0)
+        evac(3)
+        xquant(2)
+        xquant(3)
+        mm(0, 0)
+
+        left = []
+        for s in range(UNITS + 1):
+            if s == 3:
+                for g in range(PASSES):
+                    load_pair(3, g)
+            if s + 1 < UNITS:
+                inter_scalar(s + 1)
+            if 0 < s < UNITS:
+                quant(s, 0)
+                mm(s, 0)
+            if s < UNITS:
+                quant(s, 1)
+                mm(s, 1)
+            for u, m in left:
+                rot_add_store(nc.vector, u, m)
+            left = []
+            if s + 1 < UNITS:
+                inter_vector(s + 1)
+            banks = []
+            if s > 0:
+                banks.extend([(s - 1, 2), (s - 1, 3)])
+            if s < UNITS:
+                banks.extend([(s, 0), (s, 1)])
+            for u, m in banks:
+                rot_mul(u, m)
+                if (u, m) == banks[-1]:
+                    left.append((u, m))
+                else:
+                    rot_add_store(nc.gpsimd, u, m)
+        for u, m in left:
+            rot_add_store(nc.vector, u, m)

@@ -23,7 +23,19 @@ NB = 512
 UNITS = 2 * NF // NB
 FLOPS = 2 * TOK * K * 2 * NF
 
-VCOLS = (0, 512, 320, 320, 320, 320, 320, 320)
+HEAD_SPLIT = 192
+ALL_S = (("S", 0, 0, NB), ("S", 1, 0, NB), ("S", 2, 0, NB), ("S", 3, 0, NB))
+LAST_V = (("S", 0, 0, NB), ("S", 1, 0, NB), ("S", 2, 0, NB), ("V", 3, 0, NB))
+SHARE = (
+    (("S", 0, 0, NB), ("S", 2, 0, HEAD_SPLIT), ("S", 3, 0, HEAD_SPLIT)),
+    (("S", 0, 0, NB), ("S", 2, 0, NB)),
+    LAST_V,
+    LAST_V,
+    LAST_V,
+    ALL_S,
+    ALL_S,
+    ALL_S,
+)
 
 
 def tile_attention_pa_kernel(tc, x, freqs_cos, freqs_sin, wq, wk, out_0, out_1):
@@ -40,7 +52,7 @@ def tile_attention_pa_kernel(tc, x, freqs_cos, freqs_sin, wq, wk, out_0, out_1):
         raw_pool = ctx.enter_context(tc.tile_pool(name="raw", bufs=8))
         gpool = ctx.enter_context(tc.tile_pool(name="grp", bufs=4))
         cpool = ctx.enter_context(tc.tile_pool(name="codes", bufs=2))
-        rpool = ctx.enter_context(tc.tile_pool(name="prod", bufs=4))
+        rpool = ctx.enter_context(tc.tile_pool(name="prod", bufs=6))
         opool = ctx.enter_context(tc.tile_pool(name="outp", bufs=6))
         psum = ctx.enter_context(tc.psum_pool(name="psum", bufs=8))
         ctx.enter_context(tc.manual_schedule())
@@ -106,7 +118,7 @@ def tile_attention_pa_kernel(tc, x, freqs_cos, freqs_sin, wq, wk, out_0, out_1):
             t = xgpool.tile([P, K], BF16, tag="xg", align_bytes=64)
             tw = t[:].bitcast(F32).rearrange("p (g r u) -> p g r u", g=PASSES, u=2)
             for hb in range(2):
-                nc.vector.tensor_copy(
+                nc.scalar.copy(
                     out=tw[:, 2 * hb : 2 * hb + 2, :, :],
                     in_=xt[(m, hb)][:].rearrange("p (gg u) r -> p gg r u", u=2),
                 )
@@ -115,23 +127,23 @@ def tile_attention_pa_kernel(tc, x, freqs_cos, freqs_sin, wq, wk, out_0, out_1):
         def xquant(m):
             nc.vector.quantize_mx(out=x_codes[:, m, :].bitcast(E5X4), scales=x_scales[:, m, :], in_=xg[m][:])
 
-        def inter_scalar(u):
+        def new_grouped(u):
             for b in range(2):
                 t = gpool.tile([P, 2, NB, PACK], BF16, tag="grp", align_bytes=64)
                 grouped[(u, b)] = t
-                for gg in range(2):
-                    g = 2 * b + gg
-                    cs = NB - VCOLS[u] if g == PASSES - 1 else NB
-                    if cs > 0:
-                        nc.scalar.copy(out=t[:, gg, 0:cs, :], in_=raw[(u, g)][:, :, 0:cs].rearrange("p j c -> p c j"))
 
-        def inter_vector(u):
-            if VCOLS[u] > 0:
-                cs = NB - VCOLS[u]
-                nc.vector.tensor_copy(
-                    out=grouped[(u, 1)][:, 1, cs:NB, :],
-                    in_=raw[(u, PASSES - 1)][:, :, cs:NB].rearrange("p j c -> p c j"),
-                )
+        def inter(eng, u, g, c0, c1):
+            dst = grouped[(u, g // 2)][:, g % 2, c0:c1, :]
+            src = raw[(u, g)][:, :, c0:c1].rearrange("p j c -> p c j")
+            if eng == "S":
+                nc.scalar.copy(out=dst, in_=src)
+            else:
+                nc.vector.tensor_copy(out=dst, in_=src)
+
+        def inter_unit(eng, u):
+            for e, g, c0, c1 in SHARE[u]:
+                if e == eng:
+                    inter(e, u, g, c0, c1)
 
         def quant(u, b):
             if b == 0:
@@ -182,64 +194,75 @@ def tile_attention_pa_kernel(tc, x, freqs_cos, freqs_sin, wq, wk, out_0, out_1):
             )
             nc.sync.dma_start(out=outs[w][m * P : (m + 1) * P, nb * NB : (nb + 1) * NB], in_=o[:])
 
+        for m in range(MT):
+            load_x(m)
         nc.sync.dma_start(out=cos_raw[:], in_=freqs_cos.rearrange("(m p) i -> p m i", p=P))
         nc.sync.dma_start(out=sin_raw[:], in_=freqs_sin.rearrange("(m p) i -> p m i", p=P))
-        for g in range(PASSES):
-            load_half(0, g)
-            load_x(g)
-        for g in range(PASSES):
-            load_half(1, g)
+        for u in range(2):
+            for g in range(PASSES):
+                load_half(u, g)
         for cp in (1, 2):
             for g in range(PASSES):
                 load_pair(cp, g)
 
-        tabv = tab[:].rearrange("p m r (i e) -> p m r i e", e=2)
-        nc.vector.tensor_copy(out=tabv[:, :, 0, :, :], in_=cos_raw[:].unsqueeze(3).to_broadcast([P, MT, 64, 2]))
-        nc.vector.tensor_copy(out=tabv[:, :, 1, :, 0], in_=sin_raw[:])
-        nc.vector.tensor_scalar_mul(out=tabv[:, :, 1, :, 1], in0=sin_raw[:], scalar1=-1.0)
-
-        inter_scalar(0)
         for m in range(MT):
             xpose(m)
+        tabv = tab[:].rearrange("p m r (i e) -> p m r i e", e=2)
         evac(0)
         evac(1)
         xquant(0)
         evac(2)
         xquant(1)
-        quant(0, 0)
         evac(3)
         xquant(2)
+        nc.vector.tensor_copy(out=tabv[:, :, 0, :, :], in_=cos_raw[:].unsqueeze(3).to_broadcast([P, MT, 64, 2]))
         xquant(3)
+        nc.vector.tensor_copy(out=tabv[:, :, 1, :, 0], in_=sin_raw[:])
+        nc.vector.tensor_scalar_mul(out=tabv[:, :, 1, :, 1], in0=sin_raw[:], scalar1=-1.0)
+
+        new_grouped(0)
+        new_grouped(1)
+        inter_unit("S", 0)
+        inter_unit("S", 1)
+        inter("V", 0, 1, 0, NB)
+        inter("V", 0, 2, HEAD_SPLIT, NB)
+        quant(0, 0)
         mm(0, 0)
+        inter("V", 0, 3, HEAD_SPLIT, NB)
+        inter("V", 1, 1, 0, NB)
+        quant(0, 1)
+        mm(0, 1)
+        inter("V", 1, 3, 0, NB)
 
         left = []
         for s in range(UNITS + 1):
             if s == 3:
                 for g in range(PASSES):
                     load_pair(3, g)
-            if s + 1 < UNITS:
-                inter_scalar(s + 1)
+            if 2 <= s + 1 < UNITS:
+                new_grouped(s + 1)
+                inter_unit("S", s + 1)
             if 0 < s < UNITS:
                 quant(s, 0)
                 mm(s, 0)
-            if s < UNITS:
                 quant(s, 1)
                 mm(s, 1)
             for u, m in left:
                 rot_add_store(nc.vector, u, m)
             left = []
-            if s + 1 < UNITS:
-                inter_vector(s + 1)
             banks = []
             if s > 0:
                 banks.extend([(s - 1, 2), (s - 1, 3)])
             if s < UNITS:
                 banks.extend([(s, 0), (s, 1)])
-            for u, m in banks:
+            n_gpsimd = len(banks) // 2
+            for i, (u, m) in enumerate(banks):
                 rot_mul(u, m)
-                if (u, m) == banks[-1]:
-                    left.append((u, m))
-                else:
+                if i < n_gpsimd:
                     rot_add_store(nc.gpsimd, u, m)
+                else:
+                    left.append((u, m))
+            if 2 <= s + 1 < UNITS:
+                inter_unit("V", s + 1)
         for u, m in left:
             rot_add_store(nc.vector, u, m)

@@ -31,7 +31,7 @@ SHARE = (
     (("S", 0, 0, NB), ("S", 2, 0, NB)),
     LAST_V,
     LAST_V,
-    LAST_V,
+    ALL_S,
     ALL_S,
     ALL_S,
     ALL_S,
@@ -133,8 +133,8 @@ def tile_attention_pa_kernel(tc, x, freqs_cos, freqs_sin, wq, wk, out_0, out_1):
                 grouped[(u, b)] = t
 
         def inter(eng, u, g, c0, c1):
-            dst = grouped[(u, g // 2)][:, g % 2, c0:c1, :]
-            src = raw[(u, g)][:, :, c0:c1].rearrange("p j c -> p c j")
+            dst = grouped[(u, g // 2)][:, g % 2, c0:c1, :].rearrange("p (c i) j -> p c j i", i=4)
+            src = raw[(u, g)][:, :, c0:c1].rearrange("p j (c i) -> p c j i", i=4)
             if eng == "S":
                 nc.scalar.copy(out=dst, in_=src)
             else:

@@ -7,262 +7,268 @@ F32 = mybir.dt.float32
 BF16 = mybir.dt.bfloat16
 U32 = mybir.dt.uint32
 U8 = mybir.dt.uint8
-E5X4 = mybir.dt.float8_e5m2_x4
+E5M2_X4 = mybir.dt.float8_e5m2_x4
 MULT = mybir.AluOpType.mult
 ADD = mybir.AluOpType.add
 
 P = 128
-TOK = 512
+TOKENS = 512
 K = 2048
-NF = 2048
+FEATURES = 2048
+HEAD_DIM = 128
+PAIRS = HEAD_DIM // 2
 PACK = 4
-KP = P * PACK
-PASSES = K // KP
-MT = TOK // P
-NB = 512
-UNITS = 2 * NF // NB
-FLOPS = 2 * TOK * K * 2 * NF
+K_PASS = P * PACK
+PASSES = K // K_PASS
+TOKEN_TILES = TOKENS // P
+BLOCK = 512
+BLOCKS_PER_MATRIX = FEATURES // BLOCK
+BLOCKS = 2 * BLOCKS_PER_MATRIX
+HEADS_PER_BLOCK = BLOCK // HEAD_DIM
+RUN = 4
 
-HEAD_SPLIT = 192
-ALL_S = (("S", 0, 0, NB), ("S", 1, 0, NB), ("S", 2, 0, NB), ("S", 3, 0, NB))
-LAST_V = (("S", 0, 0, NB), ("S", 1, 0, NB), ("S", 2, 0, NB), ("V", 3, 0, NB))
-SHARE = (
-    (("S", 0, 0, NB), ("S", 2, 0, HEAD_SPLIT), ("S", 3, 0, HEAD_SPLIT)),
-    (("S", 0, 0, NB), ("S", 2, 0, NB)),
-    LAST_V,
-    LAST_V,
-    ALL_S,
-    ALL_S,
-    ALL_S,
-    ALL_S,
-)
+FLOPS = 2 * TOKENS * K * 2 * FEATURES
+
+VECTOR_FROM = {0: {1: 0, 2: 192, 3: 192}, 1: {1: 0, 3: 0}, 2: {3: 0}}
 
 
 def tile_attention_pa_kernel(tc, x, freqs_cos, freqs_sin, wq, wk, out_0, out_1):
     nc = tc.nc
-    x2 = x.rearrange("b s k -> (b s) k")
-    outs = [out_0.rearrange("b s h d -> (b s) (h d)"), out_1.rearrange("b s h d -> (b s) (h d)")]
-    ws = [wq, wk]
+    x_rows = x.rearrange("b s k -> (b s) k")
+    out_rows = [out_0.rearrange("b s h d -> (b s) (h d)"), out_1.rearrange("b s h d -> (b s) (h d)")]
+    weights = [wq, wk]
 
     with ExitStack() as ctx:
         const = ctx.enter_context(tc.tile_pool(name="const", bufs=1))
-        xpool = ctx.enter_context(tc.tile_pool(name="xpool", bufs=4))
-        xgpool = ctx.enter_context(tc.tile_pool(name="xgpool", bufs=2))
-        rawh_pool = ctx.enter_context(tc.tile_pool(name="rawh", bufs=8))
-        raw_pool = ctx.enter_context(tc.tile_pool(name="raw", bufs=8))
-        gpool = ctx.enter_context(tc.tile_pool(name="grp", bufs=4))
-        cpool = ctx.enter_context(tc.tile_pool(name="codes", bufs=2))
-        rpool = ctx.enter_context(tc.tile_pool(name="prod", bufs=6))
-        opool = ctx.enter_context(tc.tile_pool(name="outp", bufs=6))
+        x_pool = ctx.enter_context(tc.tile_pool(name="x_pool", bufs=TOKEN_TILES))
+        x_grouped_pool = ctx.enter_context(tc.tile_pool(name="x_grouped_pool", bufs=2))
+        single_pool = ctx.enter_context(tc.tile_pool(name="single_pool", bufs=2 * PASSES))
+        double_pool = ctx.enter_context(tc.tile_pool(name="double_pool", bufs=2 * PASSES))
+        grouped_pool = ctx.enter_context(tc.tile_pool(name="grouped_pool", bufs=4))
+        codes_pool = ctx.enter_context(tc.tile_pool(name="codes_pool", bufs=2))
+        products_pool = ctx.enter_context(tc.tile_pool(name="products_pool", bufs=6))
+        rotated_pool = ctx.enter_context(tc.tile_pool(name="rotated_pool", bufs=6))
         psum = ctx.enter_context(tc.psum_pool(name="psum", bufs=8))
         ctx.enter_context(tc.manual_schedule())
 
-        ident = const.tile([P, P], F32)
-        make_identity(nc, ident[:])
+        identity = const.tile([P, P], F32)
+        make_identity(nc, identity[:])
         warm_in = const.tile([P, 8], F32)
         warm_out = const.tile([P, 8], F32)
         nc.vector.memset(warm_in[:], 0.0)
         nc.scalar.copy(out=warm_out[:], in_=warm_in[:])
 
-        cos_raw = const.tile([P, MT, 64], BF16)
-        sin_raw = const.tile([P, MT, 64], BF16)
-        tab = const.tile([P, MT, 2, P], F32)
-        x_codes = const.tile([P, MT, KP], U32, align_bytes=64)
-        x_scales = const.tile([P, MT, KP], U8, align_bytes=64)
+        cos_bf16 = const.tile([P, TOKEN_TILES, PAIRS], BF16)
+        sin_bf16 = const.tile([P, TOKEN_TILES, PAIRS], BF16)
+        factors = const.tile([P, TOKEN_TILES, 2, HEAD_DIM], F32)
+        x_codes = const.tile([P, TOKEN_TILES, K_PASS], U32, align_bytes=64)
+        x_scales = const.tile([P, TOKEN_TILES, K_PASS], U8, align_bytes=64)
 
-        raw = {}
-        x_sb = {}
-        xt = {}
-        xg = {}
-        grouped = {}
+        x_tiles = {}
+        x_turned = {}
+        x_grouped = {}
+        w_rows = {}
+        w_grouped = {}
         w_codes = {}
         w_scales = {}
-        acc = {}
-        prod = {}
+        sums = {}
+        products = {}
 
         def load_x(m):
-            t = xpool.tile([P, K], BF16, tag="x_sb")
-            nc.sync.dma_start(out=t[:], in_=x2[m * P : (m + 1) * P, :])
-            x_sb[m] = t
+            tile = x_pool.tile([P, K], BF16, tag="x_tile")
+            nc.sync.dma_start(out=tile[:], in_=x_rows[m * P : (m + 1) * P, :])
+            x_tiles[m] = tile
 
-        def load_half(u, g):
-            t = rawh_pool.tile([P, PACK, NB], BF16, tag="rawh")
-            w, nb = divmod(u, 4)
-            nc.sync.dma_start(
-                out=t[:],
-                in_=ws[w][g * KP : (g + 1) * KP, nb * NB : (nb + 1) * NB].rearrange("(p j) n -> p j n", j=PACK),
-            )
-            raw[(u, g)] = t[:]
+        def k_rows(matrix, g, first_column, columns):
+            rows = weights[matrix][g * K_PASS : (g + 1) * K_PASS, first_column : first_column + columns]
+            return rows.rearrange("(p j) n -> p j n", j=PACK)
 
-        def load_pair(cp, g):
-            t = raw_pool.tile([P, PACK, 2 * NB], BF16, tag="raw")
-            w, c = divmod(cp, 2)
-            nc.sync.dma_start(
-                out=t[:],
-                in_=ws[w][g * KP : (g + 1) * KP, c * 2 * NB : (c + 1) * 2 * NB].rearrange("(p j) n -> p j n", j=PACK),
-            )
-            raw[(2 * cp, g)] = t[:, :, 0:NB]
-            raw[(2 * cp + 1, g)] = t[:, :, NB : 2 * NB]
+        def load_one_block(c, g):
+            tile = single_pool.tile([P, PACK, BLOCK], BF16, tag="single")
+            matrix, block = divmod(c, BLOCKS_PER_MATRIX)
+            nc.sync.dma_start(out=tile[:], in_=k_rows(matrix, g, block * BLOCK, BLOCK))
+            w_rows[(c, g)] = tile[:]
 
-        def xpose(m):
-            words = x_sb[m][:].bitcast(F32)
-            for hb in range(2):
+        def load_two_blocks(pair, g):
+            tile = double_pool.tile([P, PACK, 2 * BLOCK], BF16, tag="double")
+            matrix, half_matrix = divmod(pair, BLOCKS_PER_MATRIX // 2)
+            nc.sync.dma_start(out=tile[:], in_=k_rows(matrix, g, half_matrix * 2 * BLOCK, 2 * BLOCK))
+            w_rows[(2 * pair, g)] = tile[:, :, 0:BLOCK]
+            w_rows[(2 * pair + 1, g)] = tile[:, :, BLOCK : 2 * BLOCK]
+
+        def transpose_x(m):
+            words = x_tiles[m][:].bitcast(F32)
+            for half in range(2):
                 bank = psum.tile([P, 4, P], F32, tag="bank")
-                for gg in range(2):
-                    g = 2 * hb + gg
+                for g_in_half in range(2):
+                    g = 2 * half + g_in_half
                     for u in range(2):
-                        nc.tensor.transpose(bank[:, 2 * gg + u, :], words[:, 256 * g + u : 256 * (g + 1) : 2], ident[:])
-                xt[(m, hb)] = bank
+                        nc.tensor.transpose(
+                            bank[:, 2 * g_in_half + u, :], words[:, 256 * g + u : 256 * (g + 1) : 2], identity[:]
+                        )
+                x_turned[(m, half)] = bank
 
-        def evac(m):
-            t = xgpool.tile([P, K], BF16, tag="xg", align_bytes=64)
-            tw = t[:].bitcast(F32).rearrange("p (g r u) -> p g r u", g=PASSES, u=2)
-            for hb in range(2):
+        def copy_x_out(m):
+            tile = x_grouped_pool.tile([P, K], BF16, tag="x_grouped", align_bytes=64)
+            words = tile[:].bitcast(F32).rearrange("p (g r u) -> p g r u", g=PASSES, u=2)
+            for half in range(2):
                 nc.scalar.copy(
-                    out=tw[:, 2 * hb : 2 * hb + 2, :, :],
-                    in_=xt[(m, hb)][:].rearrange("p (gg u) r -> p gg r u", u=2),
+                    out=words[:, 2 * half : 2 * half + 2, :, :],
+                    in_=x_turned[(m, half)][:].rearrange("p (g u) r -> p g r u", u=2),
                 )
-            xg[m] = t
+            x_grouped[m] = tile
 
-        def xquant(m):
-            nc.vector.quantize_mx(out=x_codes[:, m, :].bitcast(E5X4), scales=x_scales[:, m, :], in_=xg[m][:])
+        def quantize_x(m):
+            nc.vector.quantize_mx(out=x_codes[:, m, :].bitcast(E5M2_X4), scales=x_scales[:, m, :], in_=x_grouped[m][:])
 
-        def new_grouped(u):
-            for b in range(2):
-                t = gpool.tile([P, 2, NB, PACK], BF16, tag="grp", align_bytes=64)
-                grouped[(u, b)] = t
+        def new_grouped(c):
+            for half in range(2):
+                tile = grouped_pool.tile([P, 2, BLOCK, PACK], BF16, tag="grouped", align_bytes=64)
+                w_grouped[(c, half)] = tile
 
-        def inter(eng, u, g, c0, c1):
-            dst = grouped[(u, g // 2)][:, g % 2, c0:c1, :].rearrange("p (c i) j -> p c j i", i=4)
-            src = raw[(u, g)][:, :, c0:c1].rearrange("p j (c i) -> p c j i", i=4)
-            if eng == "S":
-                nc.scalar.copy(out=dst, in_=src)
-            else:
-                nc.vector.tensor_copy(out=dst, in_=src)
-
-        def inter_unit(eng, u):
-            for e, g, c0, c1 in SHARE[u]:
-                if e == eng:
-                    inter(e, u, g, c0, c1)
-
-        def quant(u, b):
-            if b == 0:
-                wc = cpool.tile([P, PASSES, NB], U32, tag="wc", align_bytes=64)
-                wsc = cpool.tile([P, PASSES, NB], U8, tag="wsc", align_bytes=64)
-                w_codes[u] = wc
-                w_scales[u] = wsc
-            nc.vector.quantize_mx(
-                out=w_codes[u][:, 2 * b : 2 * b + 2, :].rearrange("p g c -> p (g c)").bitcast(E5X4),
-                scales=w_scales[u][:, 2 * b : 2 * b + 2, :].rearrange("p g c -> p (g c)"),
-                in_=grouped[(u, b)][:].rearrange("p g c j -> p (g c j)"),
+        def interleave(copy, c, g, first_column, end_column):
+            columns = slice(first_column, end_column)
+            copy(
+                out=w_grouped[(c, g // 2)][:, g % 2, columns, :].rearrange("p (n i) j -> p n j i", i=RUN),
+                in_=w_rows[(c, g)][:, :, columns].rearrange("p j (n i) -> p n j i", i=RUN),
             )
 
-        def mm(u, b):
-            for m in range(MT):
-                if b == 0:
-                    bank = psum.tile([P, NB], F32, tag="bank")
-                    acc[(u, m)] = bank
-                for g in (2 * b, 2 * b + 1):
+        def interleave_on_scalar(c):
+            for g in range(PASSES):
+                end_column = VECTOR_FROM.get(c, {}).get(g, BLOCK)
+                if end_column > 0:
+                    interleave(nc.scalar.copy, c, g, 0, end_column)
+
+        def interleave_on_vector(c, g):
+            interleave(nc.vector.tensor_copy, c, g, VECTOR_FROM[c][g], BLOCK)
+
+        def quantize_weights(c, half):
+            if half == 0:
+                codes = codes_pool.tile([P, PASSES, BLOCK], U32, tag="codes", align_bytes=64)
+                scales = codes_pool.tile([P, PASSES, BLOCK], U8, tag="scales", align_bytes=64)
+                w_codes[c] = codes
+                w_scales[c] = scales
+            two_passes = slice(2 * half, 2 * half + 2)
+            nc.vector.quantize_mx(
+                out=w_codes[c][:, two_passes, :].rearrange("p g n -> p (g n)").bitcast(E5M2_X4),
+                scales=w_scales[c][:, two_passes, :].rearrange("p g n -> p (g n)"),
+                in_=w_grouped[(c, half)][:].rearrange("p g n j -> p (g n j)"),
+            )
+
+        def multiply(c, half):
+            for m in range(TOKEN_TILES):
+                if half == 0:
+                    bank = psum.tile([P, BLOCK], F32, tag="bank")
+                    sums[(c, m)] = bank
+                for g in (2 * half, 2 * half + 1):
+                    tokens = slice(g * P, (g + 1) * P)
                     nc.tensor.matmul_mx(
-                        out=acc[(u, m)][:],
-                        lhsT=x_codes[:, m, g * P : (g + 1) * P].bitcast(E5X4),
-                        lhsT_scale=x_scales[:, m, g * P : (g + 1) * P],
-                        rhs=w_codes[u][:, g, :].bitcast(E5X4),
-                        rhs_scale=w_scales[u][:, g, :],
+                        out=sums[(c, m)][:],
+                        lhsT=x_codes[:, m, tokens].bitcast(E5M2_X4),
+                        lhsT_scale=x_scales[:, m, tokens],
+                        rhs=w_codes[c][:, g, :].bitcast(E5M2_X4),
+                        rhs_scale=w_scales[c][:, g, :],
                         start=(g == 0),
                         stop=(g == PASSES - 1),
                     )
 
-        def rot_mul(u, m):
-            t = rpool.tile([P, 2, NB], F32, tag="prod")
+        def quantize_and_multiply(c):
+            for half in range(2):
+                quantize_weights(c, half)
+                multiply(c, half)
+
+        def multiply_by_factors(c, m):
+            tile = products_pool.tile([P, 2, BLOCK], F32, tag="products")
+            shape = [P, 2, HEADS_PER_BLOCK, HEAD_DIM]
             nc.vector.tensor_tensor(
-                out=t[:].rearrange("p r (h j) -> p r h j", h=4),
-                in0=acc[(u, m)][:].rearrange("p (h j) -> p h j", h=4).unsqueeze(1).to_broadcast([P, 2, 4, P]),
-                in1=tab[:, m, :, :].unsqueeze(2).to_broadcast([P, 2, 4, P]),
+                out=tile[:].rearrange("p r (h d) -> p r h d", h=HEADS_PER_BLOCK),
+                in0=sums[(c, m)][:].rearrange("p (h d) -> p h d", h=HEADS_PER_BLOCK).unsqueeze(1).to_broadcast(shape),
+                in1=factors[:, m, :, :].unsqueeze(2).to_broadcast(shape),
                 op=MULT,
             )
-            prod[(u, m)] = t
+            products[(c, m)] = tile
 
-        def rot_add_store(eng, u, m):
-            w, nb = divmod(u, 4)
-            o = opool.tile([P, NB], F32, tag="o")
-            eng.tensor_tensor(
-                out=o[:].rearrange("p (n e) -> p n e", e=2),
-                in0=prod[(u, m)][:, 0, :].rearrange("p (n e) -> p n e", e=2),
-                in1=prod[(u, m)][:, 1, :].rearrange("p (n e) -> p n e", e=2)[:, :, ::-1],
+        def add_and_store(engine, c, m):
+            tile = rotated_pool.tile([P, BLOCK], F32, tag="rotated")
+            engine.tensor_tensor(
+                out=tile[:].rearrange("p (n e) -> p n e", e=2),
+                in0=products[(c, m)][:, 0, :].rearrange("p (n e) -> p n e", e=2),
+                in1=products[(c, m)][:, 1, :].rearrange("p (n e) -> p n e", e=2)[:, :, ::-1],
                 op=ADD,
             )
-            nc.sync.dma_start(out=outs[w][m * P : (m + 1) * P, nb * NB : (nb + 1) * NB], in_=o[:])
+            matrix, block = divmod(c, BLOCKS_PER_MATRIX)
+            nc.sync.dma_start(
+                out=out_rows[matrix][m * P : (m + 1) * P, block * BLOCK : (block + 1) * BLOCK], in_=tile[:]
+            )
 
-        for m in range(MT):
+        for m in range(TOKEN_TILES):
             load_x(m)
-        nc.sync.dma_start(out=cos_raw[:], in_=freqs_cos.rearrange("(m p) i -> p m i", p=P))
-        nc.sync.dma_start(out=sin_raw[:], in_=freqs_sin.rearrange("(m p) i -> p m i", p=P))
-        for u in range(2):
+        nc.sync.dma_start(out=cos_bf16[:], in_=freqs_cos.rearrange("(m p) i -> p m i", p=P))
+        nc.sync.dma_start(out=sin_bf16[:], in_=freqs_sin.rearrange("(m p) i -> p m i", p=P))
+        for c in range(2):
             for g in range(PASSES):
-                load_half(u, g)
-        for cp in (1, 2):
+                load_one_block(c, g)
+        for pair in (1, 2):
             for g in range(PASSES):
-                load_pair(cp, g)
+                load_two_blocks(pair, g)
 
-        for m in range(MT):
-            xpose(m)
-        tabv = tab[:].rearrange("p m r (i e) -> p m r i e", e=2)
-        evac(0)
-        evac(1)
-        xquant(0)
-        evac(2)
-        xquant(1)
-        evac(3)
-        xquant(2)
-        nc.vector.tensor_copy(out=tabv[:, :, 0, :, :], in_=cos_raw[:].unsqueeze(3).to_broadcast([P, MT, 64, 2]))
-        xquant(3)
-        nc.vector.tensor_copy(out=tabv[:, :, 1, :, 0], in_=sin_raw[:])
-        nc.vector.tensor_scalar_mul(out=tabv[:, :, 1, :, 1], in0=sin_raw[:], scalar1=-1.0)
+        for m in range(TOKEN_TILES):
+            transpose_x(m)
+        by_pair = factors[:].rearrange("p m r (i e) -> p m r i e", e=2)
+        copy_x_out(0)
+        copy_x_out(1)
+        quantize_x(0)
+        copy_x_out(2)
+        quantize_x(1)
+        copy_x_out(3)
+        quantize_x(2)
+        nc.vector.tensor_copy(
+            out=by_pair[:, :, 0, :, :], in_=cos_bf16[:].unsqueeze(3).to_broadcast([P, TOKEN_TILES, PAIRS, 2])
+        )
+        quantize_x(3)
+        nc.vector.tensor_copy(out=by_pair[:, :, 1, :, 0], in_=sin_bf16[:])
+        nc.vector.tensor_scalar_mul(out=by_pair[:, :, 1, :, 1], in0=sin_bf16[:], scalar1=-1.0)
 
         new_grouped(0)
         new_grouped(1)
-        inter_unit("S", 0)
-        inter_unit("S", 1)
-        inter("V", 0, 1, 0, NB)
-        inter("V", 0, 2, HEAD_SPLIT, NB)
-        quant(0, 0)
-        mm(0, 0)
-        inter("V", 0, 3, HEAD_SPLIT, NB)
-        inter("V", 1, 1, 0, NB)
-        quant(0, 1)
-        mm(0, 1)
-        inter("V", 1, 3, 0, NB)
+        interleave_on_scalar(0)
+        interleave_on_scalar(1)
+        interleave_on_vector(0, 1)
+        interleave_on_vector(0, 2)
+        quantize_weights(0, 0)
+        multiply(0, 0)
+        interleave_on_vector(0, 3)
+        interleave_on_vector(1, 1)
+        quantize_weights(0, 1)
+        multiply(0, 1)
+        interleave_on_vector(1, 3)
 
-        left = []
-        for s in range(UNITS + 1):
-            if s == 3:
+        waiting_for_vector = []
+        for c in range(BLOCKS + 1):
+            if c == 3:
                 for g in range(PASSES):
-                    load_pair(3, g)
-            if 2 <= s + 1 < UNITS:
-                new_grouped(s + 1)
-                inter_unit("S", s + 1)
-            if 0 < s < UNITS:
-                quant(s, 0)
-                mm(s, 0)
-                quant(s, 1)
-                mm(s, 1)
-            for u, m in left:
-                rot_add_store(nc.vector, u, m)
-            left = []
+                    load_two_blocks(3, g)
+            interleave_next = 2 <= c + 1 < BLOCKS
+            if interleave_next:
+                new_grouped(c + 1)
+                interleave_on_scalar(c + 1)
+            if 0 < c < BLOCKS:
+                quantize_and_multiply(c)
+            for bank in waiting_for_vector:
+                add_and_store(nc.vector, *bank)
             banks = []
-            if s > 0:
-                banks.extend([(s - 1, 2), (s - 1, 3)])
-            if s < UNITS:
-                banks.extend([(s, 0), (s, 1)])
-            n_gpsimd = len(banks) // 2
-            for i, (u, m) in enumerate(banks):
-                rot_mul(u, m)
-                if i < n_gpsimd:
-                    rot_add_store(nc.gpsimd, u, m)
-                else:
-                    left.append((u, m))
-            if 2 <= s + 1 < UNITS:
-                inter_unit("V", s + 1)
-        for u, m in left:
-            rot_add_store(nc.vector, u, m)
+            if c > 0:
+                banks.extend([(c - 1, 2), (c - 1, 3)])
+            if c < BLOCKS:
+                banks.extend([(c, 0), (c, 1)])
+            for_gpsimd = banks[: len(banks) // 2]
+            waiting_for_vector = banks[len(banks) // 2 :]
+            for bank in banks:
+                multiply_by_factors(*bank)
+                if bank in for_gpsimd:
+                    add_and_store(nc.gpsimd, *bank)
+            if interleave_next:
+                for g in sorted(VECTOR_FROM.get(c + 1, {})):
+                    interleave_on_vector(c + 1, g)
+        for bank in waiting_for_vector:
+            add_and_store(nc.vector, *bank)

@@ -29,7 +29,11 @@ RUN = 4
 
 FLOPS = 2 * TOKENS * K * 2 * FEATURES
 
-VECTOR_FROM = {0: {1: 0, 2: 192, 3: 192}, 1: {1: 0, 3: 0}, 2: {3: 0}}
+VECTOR_FROM = {0: {1: 0, 2: 192, 3: 192}, 1: {1: 0, 3: 0}}
+
+FIRST_ROUTED = 2
+HALF = 256
+ROUTED = [(2, 256), (3, 0), (3, 256)]
 
 
 def tile_attention_pa_kernel(tc, x, freqs_cos, freqs_sin, wq, wk, out_0, out_1):
@@ -48,11 +52,14 @@ def tile_attention_pa_kernel(tc, x, freqs_cos, freqs_sin, wq, wk, out_0, out_1):
         codes_pool = ctx.enter_context(tc.tile_pool(name="codes_pool", bufs=2))
         products_pool = ctx.enter_context(tc.tile_pool(name="products_pool", bufs=6))
         rotated_pool = ctx.enter_context(tc.tile_pool(name="rotated_pool", bufs=6))
-        psum = ctx.enter_context(tc.psum_pool(name="psum", bufs=8))
+        sums_pool = ctx.enter_context(tc.psum_pool(name="sums_pool", bufs=5))
+        routed_pool = ctx.enter_context(tc.psum_pool(name="routed_pool", bufs=3))
         ctx.enter_context(tc.manual_schedule())
 
         identity = const.tile([P, P], F32)
         make_identity(nc, identity[:])
+        identity_bf16 = const.tile([P, P], BF16)
+        make_identity(nc, identity_bf16[:])
         warm_in = const.tile([P, 8], F32)
         warm_out = const.tile([P, 8], F32)
         nc.vector.memset(warm_in[:], 0.0)
@@ -71,6 +78,7 @@ def tile_attention_pa_kernel(tc, x, freqs_cos, freqs_sin, wq, wk, out_0, out_1):
         w_grouped = {}
         w_codes = {}
         w_scales = {}
+        routed = {}
         sums = {}
         products = {}
 
@@ -99,7 +107,10 @@ def tile_attention_pa_kernel(tc, x, freqs_cos, freqs_sin, wq, wk, out_0, out_1):
         def transpose_x(m):
             words = x_tiles[m][:].bitcast(F32)
             for half in range(2):
-                bank = psum.tile([P, 4, P], F32, tag="bank")
+                if 2 * m + half < 5:
+                    bank = sums_pool.tile([P, 4, P], F32, tag="sums")
+                else:
+                    bank = routed_pool.tile([P, 4, P], F32, tag="routed")
                 for g_in_half in range(2):
                     g = 2 * half + g_in_half
                     for u in range(2):
@@ -136,8 +147,31 @@ def tile_attention_pa_kernel(tc, x, freqs_cos, freqs_sin, wq, wk, out_0, out_1):
         def interleave_on_scalar(c):
             for g in range(PASSES):
                 end_column = VECTOR_FROM.get(c, {}).get(g, BLOCK)
+                if c >= FIRST_ROUTED:
+                    end_column = min([first_column for routed_g, first_column in ROUTED if routed_g == g] + [BLOCK])
                 if end_column > 0:
                     interleave(nc.scalar.copy, c, g, 0, end_column)
+
+        def interleave_on_tensor(c):
+            for g, first_column in ROUTED:
+                bank = routed_pool.tile([P, 2, P, PACK], BF16, tag="routed")
+                for r in range(2):
+                    columns = slice(first_column + r * P, first_column + (r + 1) * P)
+                    nc.tensor.matmul(
+                        out=bank[:, r, :, :],
+                        lhsT=identity_bf16[:],
+                        rhs=w_rows[(c, g)][:, :, columns].rearrange("p j n -> p n j"),
+                        start=True,
+                        stop=True,
+                    )
+                routed[(c, g, first_column)] = bank
+
+        def copy_routed_out(c):
+            for g, first_column in ROUTED:
+                nc.scalar.copy(
+                    out=w_grouped[(c, g // 2)][:, g % 2, first_column : first_column + HALF, :].rearrange("p n j -> p (n j)"),
+                    in_=routed[(c, g, first_column)][:].rearrange("p r n j -> p (r n j)"),
+                )
 
         def interleave_on_vector(c, g):
             interleave(nc.vector.tensor_copy, c, g, VECTOR_FROM[c][g], BLOCK)
@@ -158,7 +192,7 @@ def tile_attention_pa_kernel(tc, x, freqs_cos, freqs_sin, wq, wk, out_0, out_1):
         def multiply(c, half):
             for m in range(TOKEN_TILES):
                 if half == 0:
-                    bank = psum.tile([P, BLOCK], F32, tag="bank")
+                    bank = sums_pool.tile([P, BLOCK], F32, tag="sums")
                     sums[(c, m)] = bank
                 for g in (2 * half, 2 * half + 1):
                     tokens = slice(g * P, (g + 1) * P)
@@ -172,10 +206,20 @@ def tile_attention_pa_kernel(tc, x, freqs_cos, freqs_sin, wq, wk, out_0, out_1):
                         stop=(g == PASSES - 1),
                     )
 
-        def quantize_and_multiply(c):
-            for half in range(2):
-                quantize_weights(c, half)
-                multiply(c, half)
+        def multiply_all_passes(c, m):
+            bank = sums_pool.tile([P, BLOCK], F32, tag="sums")
+            sums[(c, m)] = bank
+            for g in range(PASSES):
+                tokens = slice(g * P, (g + 1) * P)
+                nc.tensor.matmul_mx(
+                    out=bank[:],
+                    lhsT=x_codes[:, m, tokens].bitcast(E5M2_X4),
+                    lhsT_scale=x_scales[:, m, tokens],
+                    rhs=w_codes[c][:, g, :].bitcast(E5M2_X4),
+                    rhs_scale=w_scales[c][:, g, :],
+                    start=(g == 0),
+                    stop=(g == PASSES - 1),
+                )
 
         def multiply_by_factors(c, m):
             tile = products_pool.tile([P, 2, BLOCK], F32, tag="products")
@@ -253,7 +297,16 @@ def tile_attention_pa_kernel(tc, x, freqs_cos, freqs_sin, wq, wk, out_0, out_1):
                 new_grouped(c + 1)
                 interleave_on_scalar(c + 1)
             if 0 < c < BLOCKS:
-                quantize_and_multiply(c)
+                quantize_weights(c, 0)
+                quantize_weights(c, 1)
+                multiply_all_passes(c, 0)
+                multiply_all_passes(c, 1)
+            if interleave_next:
+                interleave_on_tensor(c + 1)
+                copy_routed_out(c + 1)
+            if 0 < c < BLOCKS:
+                multiply_all_passes(c, 2)
+                multiply_all_passes(c, 3)
             for bank in waiting_for_vector:
                 add_and_store(nc.vector, *bank)
             banks = []

@@ -26,14 +26,15 @@ BLOCKS_PER_MATRIX = FEATURES // BLOCK
 BLOCKS = 2 * BLOCKS_PER_MATRIX
 HEADS_PER_BLOCK = BLOCK // HEAD_DIM
 RUN = 4
+HALF = BLOCK // 2
 
 FLOPS = 2 * TOKENS * K * 2 * FEATURES
 
-VECTOR_FROM = {0: {1: 0, 2: 192, 3: 192}, 1: {1: 0, 3: 0}}
-
-FIRST_ROUTED = 2
-HALF = 256
-ROUTED = [(2, 256), (3, 0), (3, 256)]
+VECTOR_FROM = {0: {0: 192, 1: 192, 2: 192, 3: 192}, 1: {1: 0, 3: 0}, 2: {3: 0}}
+ROUTED = {2: [(0, 0), (0, 256)], 3: [(0, 0), (0, 256)], 4: [(0, 0), (0, 256)], 5: [(0, 0), (0, 256)], 6: [(0, 0), (0, 256)], 7: [(0, 0), (0, 256)]}
+GPSIMD_ADDS = 3
+PAIRED = [1,2,3]
+X_ON_VECTOR = []
 
 
 def tile_attention_pa_kernel(tc, x, freqs_cos, freqs_sin, wq, wk, out_0, out_1):
@@ -46,12 +47,11 @@ def tile_attention_pa_kernel(tc, x, freqs_cos, freqs_sin, wq, wk, out_0, out_1):
         const = ctx.enter_context(tc.tile_pool(name="const", bufs=1))
         x_pool = ctx.enter_context(tc.tile_pool(name="x_pool", bufs=TOKEN_TILES))
         x_grouped_pool = ctx.enter_context(tc.tile_pool(name="x_grouped_pool", bufs=2))
-        single_pool = ctx.enter_context(tc.tile_pool(name="single_pool", bufs=2 * PASSES))
-        double_pool = ctx.enter_context(tc.tile_pool(name="double_pool", bufs=2 * PASSES))
+        single_pool = ctx.enter_context(tc.tile_pool(name="single_pool", bufs=8))
+        double_pool = ctx.enter_context(tc.tile_pool(name="double_pool", bufs=8))
         grouped_pool = ctx.enter_context(tc.tile_pool(name="grouped_pool", bufs=4))
         codes_pool = ctx.enter_context(tc.tile_pool(name="codes_pool", bufs=2))
-        products_pool = ctx.enter_context(tc.tile_pool(name="products_pool", bufs=6))
-        rotated_pool = ctx.enter_context(tc.tile_pool(name="rotated_pool", bufs=6))
+        products_pool = ctx.enter_context(tc.tile_pool(name="products_pool", bufs=8))
         sums_pool = ctx.enter_context(tc.psum_pool(name="sums_pool", bufs=5))
         routed_pool = ctx.enter_context(tc.psum_pool(name="routed_pool", bufs=3))
         ctx.enter_context(tc.manual_schedule())
@@ -86,6 +86,10 @@ def tile_attention_pa_kernel(tc, x, freqs_cos, freqs_sin, wq, wk, out_0, out_1):
             tile = x_pool.tile([P, K], BF16, tag="x_tile")
             nc.sync.dma_start(out=tile[:], in_=x_rows[m * P : (m + 1) * P, :])
             x_tiles[m] = tile
+
+        def load_factors():
+            nc.sync.dma_start(out=cos_bf16[:], in_=freqs_cos.rearrange("(m p) i -> p m i", p=P))
+            nc.sync.dma_start(out=sin_bf16[:], in_=freqs_sin.rearrange("(m p) i -> p m i", p=P))
 
         def k_rows(matrix, g, first_column, columns):
             rows = weights[matrix][g * K_PASS : (g + 1) * K_PASS, first_column : first_column + columns]
@@ -123,7 +127,8 @@ def tile_attention_pa_kernel(tc, x, freqs_cos, freqs_sin, wq, wk, out_0, out_1):
             tile = x_grouped_pool.tile([P, K], BF16, tag="x_grouped", align_bytes=64)
             words = tile[:].bitcast(F32).rearrange("p (g r u) -> p g r u", g=PASSES, u=2)
             for half in range(2):
-                nc.scalar.copy(
+                copy = nc.vector.tensor_copy if (m, half) in X_ON_VECTOR else nc.scalar.copy
+                copy(
                     out=words[:, 2 * half : 2 * half + 2, :, :],
                     in_=x_turned[(m, half)][:].rearrange("p (g u) r -> p g r u", u=2),
                 )
@@ -131,6 +136,14 @@ def tile_attention_pa_kernel(tc, x, freqs_cos, freqs_sin, wq, wk, out_0, out_1):
 
         def quantize_x(m):
             nc.vector.quantize_mx(out=x_codes[:, m, :].bitcast(E5M2_X4), scales=x_scales[:, m, :], in_=x_grouped[m][:])
+
+        def widen_factors():
+            by_pair = factors[:].rearrange("p m r (i e) -> p m r i e", e=2)
+            nc.vector.tensor_copy(
+                out=by_pair[:, :, 0, :, :], in_=cos_bf16[:].unsqueeze(3).to_broadcast([P, TOKEN_TILES, PAIRS, 2])
+            )
+            nc.vector.tensor_copy(out=by_pair[:, :, 1, :, 0], in_=sin_bf16[:])
+            nc.vector.tensor_scalar_mul(out=by_pair[:, :, 1, :, 1], in0=sin_bf16[:], scalar1=-1.0)
 
         def new_grouped(c):
             for half in range(2):
@@ -144,16 +157,18 @@ def tile_attention_pa_kernel(tc, x, freqs_cos, freqs_sin, wq, wk, out_0, out_1):
                 in_=w_rows[(c, g)][:, :, columns].rearrange("p j (n i) -> p n j i", i=RUN),
             )
 
-        def interleave_on_scalar(c):
-            for g in range(PASSES):
-                end_column = VECTOR_FROM.get(c, {}).get(g, BLOCK)
-                if c >= FIRST_ROUTED:
-                    end_column = min([first_column for routed_g, first_column in ROUTED if routed_g == g] + [BLOCK])
-                if end_column > 0:
-                    interleave(nc.scalar.copy, c, g, 0, end_column)
+        def interleave_on_scalar(c, g):
+            first_column = HALF * len([1 for routed_g, column in ROUTED.get(c, []) if routed_g == g])
+            end_column = VECTOR_FROM.get(c, {}).get(g, BLOCK)
+            if end_column > first_column:
+                interleave(nc.scalar.copy, c, g, first_column, end_column)
+
+        def interleave_on_vector(c, g):
+            if g in VECTOR_FROM.get(c, {}):
+                interleave(nc.vector.tensor_copy, c, g, VECTOR_FROM[c][g], BLOCK)
 
         def interleave_on_tensor(c):
-            for g, first_column in ROUTED:
+            for g, first_column in ROUTED.get(c, []):
                 bank = routed_pool.tile([P, 2, P, PACK], BF16, tag="routed")
                 for r in range(2):
                     columns = slice(first_column + r * P, first_column + (r + 1) * P)
@@ -167,14 +182,11 @@ def tile_attention_pa_kernel(tc, x, freqs_cos, freqs_sin, wq, wk, out_0, out_1):
                 routed[(c, g, first_column)] = bank
 
         def copy_routed_out(c):
-            for g, first_column in ROUTED:
+            for g, first_column in ROUTED.get(c, []):
                 nc.scalar.copy(
                     out=w_grouped[(c, g // 2)][:, g % 2, first_column : first_column + HALF, :].rearrange("p n j -> p (n j)"),
                     in_=routed[(c, g, first_column)][:].rearrange("p r n j -> p (r n j)"),
                 )
-
-        def interleave_on_vector(c, g):
-            interleave(nc.vector.tensor_copy, c, g, VECTOR_FROM[c][g], BLOCK)
 
         def quantize_weights(c, half):
             if half == 0:
@@ -189,30 +201,14 @@ def tile_attention_pa_kernel(tc, x, freqs_cos, freqs_sin, wq, wk, out_0, out_1):
                 in_=w_grouped[(c, half)][:].rearrange("p g n j -> p (g n j)"),
             )
 
-        def multiply(c, half):
-            for m in range(TOKEN_TILES):
-                if half == 0:
-                    bank = sums_pool.tile([P, BLOCK], F32, tag="sums")
-                    sums[(c, m)] = bank
-                for g in (2 * half, 2 * half + 1):
-                    tokens = slice(g * P, (g + 1) * P)
-                    nc.tensor.matmul_mx(
-                        out=sums[(c, m)][:],
-                        lhsT=x_codes[:, m, tokens].bitcast(E5M2_X4),
-                        lhsT_scale=x_scales[:, m, tokens],
-                        rhs=w_codes[c][:, g, :].bitcast(E5M2_X4),
-                        rhs_scale=w_scales[c][:, g, :],
-                        start=(g == 0),
-                        stop=(g == PASSES - 1),
-                    )
-
-        def multiply_all_passes(c, m):
-            bank = sums_pool.tile([P, BLOCK], F32, tag="sums")
-            sums[(c, m)] = bank
-            for g in range(PASSES):
+        def multiply(c, m, passes):
+            if passes[0] == 0:
+                bank = sums_pool.tile([P, BLOCK], F32, tag="sums")
+                sums[(c, m)] = bank
+            for g in passes:
                 tokens = slice(g * P, (g + 1) * P)
                 nc.tensor.matmul_mx(
-                    out=bank[:],
+                    out=sums[(c, m)][:],
                     lhsT=x_codes[:, m, tokens].bitcast(E5M2_X4),
                     lhsT_scale=x_scales[:, m, tokens],
                     rhs=w_codes[c][:, g, :].bitcast(E5M2_X4),
@@ -232,96 +228,96 @@ def tile_attention_pa_kernel(tc, x, freqs_cos, freqs_sin, wq, wk, out_0, out_1):
             )
             products[(c, m)] = tile
 
-        def add_and_store(engine, c, m):
-            tile = rotated_pool.tile([P, BLOCK], F32, tag="rotated")
+        def add_and_store(engine, c, m, result=None):
+            if result is None:
+                result = products[(c, m)][:, 0, :]
             engine.tensor_tensor(
-                out=tile[:].rearrange("p (n e) -> p n e", e=2),
+                out=result.rearrange("p (n e) -> p n e", e=2),
                 in0=products[(c, m)][:, 0, :].rearrange("p (n e) -> p n e", e=2),
                 in1=products[(c, m)][:, 1, :].rearrange("p (n e) -> p n e", e=2)[:, :, ::-1],
                 op=ADD,
             )
             matrix, block = divmod(c, BLOCKS_PER_MATRIX)
-            nc.sync.dma_start(
-                out=out_rows[matrix][m * P : (m + 1) * P, block * BLOCK : (block + 1) * BLOCK], in_=tile[:]
-            )
+            nc.sync.dma_start(out=out_rows[matrix][m * P : (m + 1) * P, block * BLOCK : (block + 1) * BLOCK], in_=result)
 
         for m in range(TOKEN_TILES):
             load_x(m)
-        nc.sync.dma_start(out=cos_bf16[:], in_=freqs_cos.rearrange("(m p) i -> p m i", p=P))
-        nc.sync.dma_start(out=sin_bf16[:], in_=freqs_sin.rearrange("(m p) i -> p m i", p=P))
-        for c in range(2):
+            load_one_block(0, m)
+        load_factors()
+        for c in [1]:
             for g in range(PASSES):
                 load_one_block(c, g)
-        for pair in (1, 2):
+        for pair in [1, 2]:
             for g in range(PASSES):
                 load_two_blocks(pair, g)
 
         for m in range(TOKEN_TILES):
             transpose_x(m)
-        by_pair = factors[:].rearrange("p m r (i e) -> p m r i e", e=2)
-        copy_x_out(0)
-        copy_x_out(1)
-        quantize_x(0)
-        copy_x_out(2)
-        quantize_x(1)
-        copy_x_out(3)
-        quantize_x(2)
-        nc.vector.tensor_copy(
-            out=by_pair[:, :, 0, :, :], in_=cos_bf16[:].unsqueeze(3).to_broadcast([P, TOKEN_TILES, PAIRS, 2])
-        )
-        quantize_x(3)
-        nc.vector.tensor_copy(out=by_pair[:, :, 1, :, 0], in_=sin_bf16[:])
-        nc.vector.tensor_scalar_mul(out=by_pair[:, :, 1, :, 1], in0=sin_bf16[:], scalar1=-1.0)
-
         new_grouped(0)
-        new_grouped(1)
-        interleave_on_scalar(0)
-        interleave_on_scalar(1)
-        interleave_on_vector(0, 1)
-        interleave_on_vector(0, 2)
-        quantize_weights(0, 0)
-        multiply(0, 0)
-        interleave_on_vector(0, 3)
-        interleave_on_vector(1, 1)
+        for m in range(TOKEN_TILES):
+            copy_x_out(m)
+            interleave_on_scalar(0, m)
+            interleave_on_vector(0, m)
+            quantize_x(m)
+            if m == 1:
+                quantize_weights(0, 0)
+        widen_factors()
         quantize_weights(0, 1)
-        multiply(0, 1)
-        interleave_on_vector(1, 3)
+        for m in range(TOKEN_TILES):
+            multiply(0, m, [0, 1])
+        for m in range(TOKEN_TILES):
+            multiply(0, m, [2, 3])
+        interleave_on_tensor(1)
 
-        waiting_for_vector = []
+        all_passes = list(range(PASSES))
+        previous = []
         for c in range(BLOCKS + 1):
-            if c == 3:
+            following = c + 1
+            if following < BLOCKS:
+                new_grouped(following)
+                copy_routed_out(following)
                 for g in range(PASSES):
-                    load_two_blocks(3, g)
-            interleave_next = 2 <= c + 1 < BLOCKS
-            if interleave_next:
-                new_grouped(c + 1)
-                interleave_on_scalar(c + 1)
+                    interleave_on_scalar(following, g)
+            early = [0, 1]
+            if c == 0:
+                for g in early:
+                    interleave_on_vector(1, g)
             if 0 < c < BLOCKS:
                 quantize_weights(c, 0)
                 quantize_weights(c, 1)
-                multiply_all_passes(c, 0)
-                multiply_all_passes(c, 1)
-            if interleave_next:
-                interleave_on_tensor(c + 1)
-                copy_routed_out(c + 1)
+                multiply(c, 0, all_passes)
+                multiply(c, 1, all_passes)
+            if c + 2 < BLOCKS:
+                interleave_on_tensor(c + 2)
             if 0 < c < BLOCKS:
-                multiply_all_passes(c, 2)
-                multiply_all_passes(c, 3)
-            for bank in waiting_for_vector:
+                multiply(c, 2, all_passes)
+                multiply(c, 3, all_passes)
+            count = min(GPSIMD_ADDS if c < BLOCKS else 2, max(len(previous) - 1, 0))
+            for_vector = previous[: len(previous) - count]
+            for_gpsimd = previous[len(previous) - count :]
+            for bank in for_vector:
                 add_and_store(nc.vector, *bank)
             banks = []
             if c > 0:
                 banks.extend([(c - 1, 2), (c - 1, 3)])
             if c < BLOCKS:
                 banks.extend([(c, 0), (c, 1)])
-            for_gpsimd = banks[: len(banks) // 2]
-            waiting_for_vector = banks[len(banks) // 2 :]
-            for bank in banks:
+            for i, bank in enumerate(banks):
                 multiply_by_factors(*bank)
-                if bank in for_gpsimd:
-                    add_and_store(nc.gpsimd, *bank)
-            if interleave_next:
-                for g in sorted(VECTOR_FROM.get(c + 1, {})):
-                    interleave_on_vector(c + 1, g)
-        for bank in waiting_for_vector:
+                if i < len(for_gpsimd):
+                    add_and_store(nc.gpsimd, *for_gpsimd[i], result=products[for_vector[-1]][:, 1, :] if i == 0 else None)
+            for bank in for_gpsimd[len(banks) :]:
+                add_and_store(nc.gpsimd, *bank)
+            if following < BLOCKS:
+                for g in range(PASSES):
+                    if not (c == 0 and g in early):
+                        interleave_on_vector(following, g)
+            for late_c in {}.get(c, []):
+                for g in range(PASSES):
+                    load_one_block(late_c, g)
+            for late_pair in {2: [3]}.get(c, []):
+                for g in range(PASSES):
+                    load_two_blocks(late_pair, g)
+            previous = banks
+        for bank in previous:
             add_and_store(nc.vector, *bank)

@@ -30,8 +30,10 @@ HALF = BLOCK // 2
 
 FLOPS = 2 * TOKENS * K * 2 * FEATURES
 
-VECTOR_FROM = {0: {0: 192, 1: 192, 2: 192, 3: 192}, 1: {1: 0, 3: 0}, 2: {3: 0}}
-ROUTED = {2: [(0, 0), (0, 256)], 3: [(0, 0), (0, 256)], 4: [(0, 0), (0, 256)], 5: [(0, 0), (0, 256)], 6: [(0, 0), (0, 256)], 7: [(0, 0), (0, 256)]}
+VECTOR_FROM = {0: {0: 192, 1: 192, 2: 192, 3: 192}, 1: {1: 0, 3: 256}, 2: {3: 0}}
+ROUTED = {3: [(0, 0), (0, 256)], 4: [(0, 0), (0, 256)], 5: [(0, 0), (0, 256)], 6: [(0, 0), (0, 256)], 7: [(0, 0), (0, 256)]}
+ROUTED_LATE = {7: [(3, 0), (3, 256)]}
+GPSIMD_TILES = {}
 GPSIMD_ADDS = 3
 PAIRED = [1,2,3]
 X_ON_VECTOR = []
@@ -158,17 +160,28 @@ def tile_attention_pa_kernel(tc, x, freqs_cos, freqs_sin, wq, wk, out_0, out_1):
             )
 
         def interleave_on_scalar(c, g):
-            first_column = HALF * len([1 for routed_g, column in ROUTED.get(c, []) if routed_g == g])
-            end_column = VECTOR_FROM.get(c, {}).get(g, BLOCK)
-            if end_column > first_column:
+            taken = [column for routed_g, column in ROUTED.get(c, []) + ROUTED_LATE.get(c, []) if routed_g == g]
+            first_column = HALF * len([column for column in taken if column == 0 or len(taken) == 2])
+            end_column = min([column for column in taken if column > 0 and len(taken) == 1] + [VECTOR_FROM.get(c, {}).get(g, BLOCK)])
+            if end_column > first_column and g not in GPSIMD_TILES.get(c, []):
                 interleave(nc.scalar.copy, c, g, first_column, end_column)
 
         def interleave_on_vector(c, g):
             if g in VECTOR_FROM.get(c, {}):
                 interleave(nc.vector.tensor_copy, c, g, VECTOR_FROM[c][g], BLOCK)
 
-        def interleave_on_tensor(c):
-            for g, first_column in ROUTED.get(c, []):
+        def interleave_on_gpsimd(c, g):
+            nc.gpsimd.tensor_scalar(
+                out=w_grouped[(c, g // 2)][:, g % 2, :, :],
+                in0=w_rows[(c, g)].rearrange("p j n -> p n j"),
+                scalar1=1.0,
+                scalar2=0.0,
+                op0=MULT,
+                op1=ADD,
+            )
+
+        def interleave_on_tensor(c, plan):
+            for g, first_column in plan.get(c, []):
                 bank = routed_pool.tile([P, 2, P, PACK], BF16, tag="routed")
                 for r in range(2):
                     columns = slice(first_column + r * P, first_column + (r + 1) * P)
@@ -181,8 +194,8 @@ def tile_attention_pa_kernel(tc, x, freqs_cos, freqs_sin, wq, wk, out_0, out_1):
                     )
                 routed[(c, g, first_column)] = bank
 
-        def copy_routed_out(c):
-            for g, first_column in ROUTED.get(c, []):
+        def copy_routed_out(c, plan):
+            for g, first_column in plan.get(c, []):
                 nc.scalar.copy(
                     out=w_grouped[(c, g // 2)][:, g % 2, first_column : first_column + HALF, :].rearrange("p n j -> p (n j)"),
                     in_=routed[(c, g, first_column)][:].rearrange("p r n j -> p (r n j)"),
@@ -244,9 +257,8 @@ def tile_attention_pa_kernel(tc, x, freqs_cos, freqs_sin, wq, wk, out_0, out_1):
             load_x(m)
             load_one_block(0, m)
         load_factors()
-        for c in [1]:
-            for g in range(PASSES):
-                load_one_block(c, g)
+        for g in range(PASSES):
+            load_one_block(1, g)
         for pair in [1, 2]:
             for g in range(PASSES):
                 load_two_blocks(pair, g)
@@ -267,7 +279,6 @@ def tile_attention_pa_kernel(tc, x, freqs_cos, freqs_sin, wq, wk, out_0, out_1):
             multiply(0, m, [0, 1])
         for m in range(TOKEN_TILES):
             multiply(0, m, [2, 3])
-        interleave_on_tensor(1)
 
         all_passes = list(range(PASSES))
         previous = []
@@ -275,20 +286,20 @@ def tile_attention_pa_kernel(tc, x, freqs_cos, freqs_sin, wq, wk, out_0, out_1):
             following = c + 1
             if following < BLOCKS:
                 new_grouped(following)
-                copy_routed_out(following)
+                copy_routed_out(following, ROUTED)
                 for g in range(PASSES):
                     interleave_on_scalar(following, g)
-            early = [0, 1]
             if c == 0:
-                for g in early:
+                for g in [0, 1]:
                     interleave_on_vector(1, g)
             if 0 < c < BLOCKS:
                 quantize_weights(c, 0)
                 quantize_weights(c, 1)
                 multiply(c, 0, all_passes)
                 multiply(c, 1, all_passes)
-            if c + 2 < BLOCKS:
-                interleave_on_tensor(c + 2)
+            interleave_on_tensor(c + 2, ROUTED)
+            interleave_on_tensor(c + 1, ROUTED_LATE)
+            copy_routed_out(c + 1, ROUTED_LATE)
             if 0 < c < BLOCKS:
                 multiply(c, 2, all_passes)
                 multiply(c, 3, all_passes)
@@ -306,15 +317,15 @@ def tile_attention_pa_kernel(tc, x, freqs_cos, freqs_sin, wq, wk, out_0, out_1):
                 multiply_by_factors(*bank)
                 if i < len(for_gpsimd):
                     add_and_store(nc.gpsimd, *for_gpsimd[i], result=products[for_vector[-1]][:, 1, :] if i == 0 else None)
+                if i == len(for_gpsimd):
+                    for g in GPSIMD_TILES.get(following, []):
+                        interleave_on_gpsimd(following, g)
             for bank in for_gpsimd[len(banks) :]:
                 add_and_store(nc.gpsimd, *bank)
             if following < BLOCKS:
                 for g in range(PASSES):
-                    if not (c == 0 and g in early):
+                    if not (c == 0 and g in [0, 1]):
                         interleave_on_vector(following, g)
-            for late_c in {}.get(c, []):
-                for g in range(PASSES):
-                    load_one_block(late_c, g)
             for late_pair in {2: [3]}.get(c, []):
                 for g in range(PASSES):
                     load_two_blocks(late_pair, g)

@@ -53,7 +53,7 @@ def tile_attention_pa_kernel(tc, x, freqs_cos, freqs_sin, wq, wk, out_0, out_1):
         double_pool = ctx.enter_context(tc.tile_pool(name="double_pool", bufs=8))
         grouped_pool = ctx.enter_context(tc.tile_pool(name="grouped_pool", bufs=4))
         codes_pool = ctx.enter_context(tc.tile_pool(name="codes_pool", bufs=2))
-        products_pool = ctx.enter_context(tc.tile_pool(name="products_pool", bufs=8))
+        products_pool = ctx.enter_context(tc.tile_pool(name="products_pool", bufs=3))
         sums_pool = ctx.enter_context(tc.psum_pool(name="sums_pool", bufs=5))
         routed_pool = ctx.enter_context(tc.psum_pool(name="routed_pool", bufs=3))
         ctx.enter_context(tc.manual_schedule())
@@ -230,26 +230,24 @@ def tile_attention_pa_kernel(tc, x, freqs_cos, freqs_sin, wq, wk, out_0, out_1):
                     stop=(g == PASSES - 1),
                 )
 
-        def multiply_by_factors(c, m):
-            tile = products_pool.tile([P, 2, BLOCK], F32, tag="products")
+        def multiply_by_factors(c, m, tile, slot):
             shape = [P, 2, HEADS_PER_BLOCK, HEAD_DIM]
             nc.vector.tensor_tensor(
-                out=tile[:].rearrange("p r (h d) -> p r h d", h=HEADS_PER_BLOCK),
+                out=tile[:, slot, :, :].rearrange("p r (h d) -> p r h d", h=HEADS_PER_BLOCK),
                 in0=sums[(c, m)][:].rearrange("p (h d) -> p h d", h=HEADS_PER_BLOCK).unsqueeze(1).to_broadcast(shape),
                 in1=factors[:, m, :, :].unsqueeze(2).to_broadcast(shape),
                 op=MULT,
             )
-            products[(c, m)] = tile
 
-        def add_and_store(engine, c, m, result=None):
-            if result is None:
-                result = products[(c, m)][:, 0, :]
+        def add(engine, tile, first, end, result):
             engine.tensor_tensor(
-                out=result.rearrange("p (n e) -> p n e", e=2),
-                in0=products[(c, m)][:, 0, :].rearrange("p (n e) -> p n e", e=2),
-                in1=products[(c, m)][:, 1, :].rearrange("p (n e) -> p n e", e=2)[:, :, ::-1],
+                out=result.rearrange("p b (n e) -> p b n e", e=2),
+                in0=tile[:, first:end, 0, :].rearrange("p b (n e) -> p b n e", e=2),
+                in1=tile[:, first:end, 1, :].rearrange("p b (n e) -> p b n e", e=2)[:, :, :, ::-1],
                 op=ADD,
             )
+
+        def store(c, m, result):
             matrix, block = divmod(c, BLOCKS_PER_MATRIX)
             nc.sync.dma_start(out=out_rows[matrix][m * P : (m + 1) * P, block * BLOCK : (block + 1) * BLOCK], in_=result)
 
@@ -282,6 +280,7 @@ def tile_attention_pa_kernel(tc, x, freqs_cos, freqs_sin, wq, wk, out_0, out_1):
 
         all_passes = list(range(PASSES))
         previous = []
+        previous_tile = None
         for c in range(BLOCKS + 1):
             following = c + 1
             if following < BLOCKS:
@@ -303,25 +302,23 @@ def tile_attention_pa_kernel(tc, x, freqs_cos, freqs_sin, wq, wk, out_0, out_1):
             if 0 < c < BLOCKS:
                 multiply(c, 2, all_passes)
                 multiply(c, 3, all_passes)
-            count = min(GPSIMD_ADDS if c < BLOCKS else 2, max(len(previous) - 1, 0))
-            for_vector = previous[: len(previous) - count]
-            for_gpsimd = previous[len(previous) - count :]
-            for bank in for_vector:
-                add_and_store(nc.vector, *bank)
+            count = min(GPSIMD_ADDS if c < BLOCKS else 1, max(len(previous) - 1, 0))
+            on_vector = len(previous) - count
+            for slot in range(on_vector):
+                add(nc.vector, previous_tile, slot, slot + 1, previous_tile[:, slot : slot + 1, 0, :])
+                store(*previous[slot], previous_tile[:, slot, 0, :])
             banks = []
             if c > 0:
                 banks.extend([(c - 1, 2), (c - 1, 3)])
             if c < BLOCKS:
                 banks.extend([(c, 0), (c, 1)])
-            for i, bank in enumerate(banks):
-                multiply_by_factors(*bank)
-                if i < len(for_gpsimd):
-                    add_and_store(nc.gpsimd, *for_gpsimd[i], result=products[for_vector[-1]][:, 1, :] if i == 0 else None)
-                if i == len(for_gpsimd):
-                    for g in GPSIMD_TILES.get(following, []):
-                        interleave_on_gpsimd(following, g)
-            for bank in for_gpsimd[len(banks) :]:
-                add_and_store(nc.gpsimd, *bank)
+            tile = products_pool.tile([P, 4, 2, BLOCK], F32, tag="products")
+            for slot, bank in enumerate(banks):
+                multiply_by_factors(*bank, tile, slot)
+                if slot == 0 and count > 0:
+                    add(nc.gpsimd, previous_tile, on_vector, len(previous), previous_tile[:, on_vector - 1 : len(previous) - 1, 1, :])
+                    for s in range(on_vector, len(previous)):
+                        store(*previous[s], previous_tile[:, s - 1, 1, :])
             if following < BLOCKS:
                 for g in range(PASSES):
                     if not (c == 0 and g in [0, 1]):
@@ -330,5 +327,7 @@ def tile_attention_pa_kernel(tc, x, freqs_cos, freqs_sin, wq, wk, out_0, out_1):
                 for g in range(PASSES):
                     load_two_blocks(late_pair, g)
             previous = banks
-        for bank in previous:
-            add_and_store(nc.vector, *bank)
+            previous_tile = tile
+        for slot in range(len(previous)):
+            add(nc.vector, previous_tile, slot, slot + 1, previous_tile[:, slot : slot + 1, 0, :])
+            store(*previous[slot], previous_tile[:, slot, 0, :])

@@ -90,8 +90,8 @@ def tile_attention_pa_kernel(tc, x, freqs_cos, freqs_sin, wq, wk, out_0, out_1):
             x_tiles[m] = tile
 
         def load_factors():
-            nc.sync.dma_start(out=cos_bf16[:], in_=freqs_cos.rearrange("(m p) i -> p m i", p=P))
-            nc.sync.dma_start(out=sin_bf16[:], in_=freqs_sin.rearrange("(m p) i -> p m i", p=P))
+            nc.scalar.dma_start(out=cos_bf16[:], in_=freqs_cos.rearrange("(m p) i -> p m i", p=P))
+            nc.scalar.dma_start(out=sin_bf16[:], in_=freqs_sin.rearrange("(m p) i -> p m i", p=P))
 
         def k_rows(matrix, g, first_column, columns):
             rows = weights[matrix][g * K_PASS : (g + 1) * K_PASS, first_column : first_column + columns]
@@ -141,11 +141,11 @@ def tile_attention_pa_kernel(tc, x, freqs_cos, freqs_sin, wq, wk, out_0, out_1):
 
         def widen_factors():
             by_pair = factors[:].rearrange("p m r (i e) -> p m r i e", e=2)
-            nc.vector.tensor_copy(
+            nc.scalar.copy(
                 out=by_pair[:, :, 0, :, :], in_=cos_bf16[:].unsqueeze(3).to_broadcast([P, TOKEN_TILES, PAIRS, 2])
             )
-            nc.vector.tensor_copy(out=by_pair[:, :, 1, :, 0], in_=sin_bf16[:])
-            nc.vector.tensor_scalar_mul(out=by_pair[:, :, 1, :, 1], in0=sin_bf16[:], scalar1=-1.0)
+            nc.scalar.copy(out=by_pair[:, :, 1, :, 0], in_=sin_bf16[:])
+            nc.scalar.mul(out=by_pair[:, :, 1, :, 1], in_=sin_bf16[:], mul=-1.0)
 
         def new_grouped(c):
             for half in range(2):
@@ -239,7 +239,9 @@ def tile_attention_pa_kernel(tc, x, freqs_cos, freqs_sin, wq, wk, out_0, out_1):
                 op=MULT,
             )
 
-        def add(engine, tile, first, end, result):
+        def add(engine, tile, first, end, result=None):
+            if result is None:
+                result = tile[:, first:end, 0, :]
             engine.tensor_tensor(
                 out=result.rearrange("p b (n e) -> p b n e", e=2),
                 in0=tile[:, first:end, 0, :].rearrange("p b (n e) -> p b n e", e=2),
@@ -251,16 +253,17 @@ def tile_attention_pa_kernel(tc, x, freqs_cos, freqs_sin, wq, wk, out_0, out_1):
             matrix, block = divmod(c, BLOCKS_PER_MATRIX)
             nc.sync.dma_start(out=out_rows[matrix][m * P : (m + 1) * P, block * BLOCK : (block + 1) * BLOCK], in_=result)
 
+        load_factors()
         for m in range(TOKEN_TILES):
             load_x(m)
             load_one_block(0, m)
-        load_factors()
         for g in range(PASSES):
             load_one_block(1, g)
         for pair in [1, 2]:
             for g in range(PASSES):
                 load_two_blocks(pair, g)
 
+        widen_factors()
         for m in range(TOKEN_TILES):
             transpose_x(m)
         new_grouped(0)
@@ -271,7 +274,6 @@ def tile_attention_pa_kernel(tc, x, freqs_cos, freqs_sin, wq, wk, out_0, out_1):
             quantize_x(m)
             if m == 1:
                 quantize_weights(0, 0)
-        widen_factors()
         quantize_weights(0, 1)
         for m in range(TOKEN_TILES):
             multiply(0, m, [0, 1])
@@ -302,11 +304,14 @@ def tile_attention_pa_kernel(tc, x, freqs_cos, freqs_sin, wq, wk, out_0, out_1):
             if 0 < c < BLOCKS:
                 multiply(c, 2, all_passes)
                 multiply(c, 3, all_passes)
-            count = min(GPSIMD_ADDS if c < BLOCKS else 1, max(len(previous) - 1, 0))
-            on_vector = len(previous) - count
-            for slot in range(on_vector):
-                add(nc.vector, previous_tile, slot, slot + 1, previous_tile[:, slot : slot + 1, 0, :])
-                store(*previous[slot], previous_tile[:, slot, 0, :])
+            on_gpsimd = min(3, len(previous)) if c < BLOCKS else 2
+            on_vector = len(previous) - on_gpsimd
+            if c < BLOCKS:
+                for slot in range(on_vector):
+                    add(nc.vector, previous_tile, slot, slot + 1)
+                    store(*previous[slot], previous_tile[:, slot, 0, :])
+                if on_vector == 0 and on_gpsimd > 0:
+                    nc.vector.tensor_copy(out=previous_tile[:, 0, 1, 0:2], in_=previous_tile[:, 0, 1, 0:2])
             banks = []
             if c > 0:
                 banks.extend([(c - 1, 2), (c - 1, 3)])
@@ -315,10 +320,20 @@ def tile_attention_pa_kernel(tc, x, freqs_cos, freqs_sin, wq, wk, out_0, out_1):
             tile = products_pool.tile([P, 4, 2, BLOCK], F32, tag="products")
             for slot, bank in enumerate(banks):
                 multiply_by_factors(*bank, tile, slot)
-                if slot == 0 and count > 0:
-                    add(nc.gpsimd, previous_tile, on_vector, len(previous), previous_tile[:, on_vector - 1 : len(previous) - 1, 1, :])
-                    for s in range(on_vector, len(previous)):
-                        store(*previous[s], previous_tile[:, s - 1, 1, :])
+                if slot == 0 and on_gpsimd > 0:
+                    first = on_vector if c < BLOCKS else 0
+                    if c < BLOCKS and on_vector > 0:
+                        add(nc.gpsimd, previous_tile, first, first + on_gpsimd, previous_tile[:, first - 1 : first + on_gpsimd - 1, 1, :])
+                        for s in range(first, first + on_gpsimd):
+                            store(*previous[s], previous_tile[:, s - 1, 1, :])
+                    else:
+                        add(nc.gpsimd, previous_tile, first, first + on_gpsimd)
+                        for s in range(first, first + on_gpsimd):
+                            store(*previous[s], previous_tile[:, s, 0, :])
+            if c == BLOCKS and on_vector > 0:
+                add(nc.vector, previous_tile, on_gpsimd, len(previous))
+                for s in range(on_gpsimd, len(previous)):
+                    store(*previous[s], previous_tile[:, s, 0, :])
             if following < BLOCKS:
                 for g in range(PASSES):
                     if not (c == 0 and g in [0, 1]):
@@ -329,5 +344,5 @@ def tile_attention_pa_kernel(tc, x, freqs_cos, freqs_sin, wq, wk, out_0, out_1):
             previous = banks
             previous_tile = tile
         for slot in range(len(previous)):
-            add(nc.vector, previous_tile, slot, slot + 1, previous_tile[:, slot : slot + 1, 0, :])
+            add(nc.vector, previous_tile, slot, slot + 1)
             store(*previous[slot], previous_tile[:, slot, 0, :])

@@ -30,10 +30,10 @@ HALF = BLOCK // 2
 
 FLOPS = 2 * TOKENS * K * 2 * FEATURES
 
-VECTOR_FROM = {0: {0: 192, 1: 192, 2: 192, 3: 192}, 1: {1: 0, 3: 256}, 2: {3: 0}}
+VECTOR_FROM = {0: {0: 192, 1: 192, 2: 192, 3: 192}, 1: {1: 248, 3: 256}, 2: {3: 0}}
 ROUTED = {3: [(0, 0), (0, 256)], 4: [(0, 0), (0, 256)], 5: [(0, 0), (0, 256)], 6: [(0, 0), (0, 256)], 7: [(0, 0), (0, 256)]}
 ROUTED_LATE = {7: [(3, 0), (3, 256)]}
-GPSIMD_TILES = {}
+GPSIMD_PIECES = {(1, 1): (0, 256), (2, 0): (352, 512)}
 GPSIMD_ADDS = 3
 PAIRED = [1,2,3]
 X_ON_VECTOR = []
@@ -47,7 +47,7 @@ def tile_attention_pa_kernel(tc, x, freqs_cos, freqs_sin, wq, wk, out_0, out_1):
 
     with ExitStack() as ctx:
         const = ctx.enter_context(tc.tile_pool(name="const", bufs=1))
-        x_pool = ctx.enter_context(tc.tile_pool(name="x_pool", bufs=TOKEN_TILES))
+        shared_pool = ctx.enter_context(tc.tile_pool(name="shared_pool", bufs=1))
         x_grouped_pool = ctx.enter_context(tc.tile_pool(name="x_grouped_pool", bufs=2))
         single_pool = ctx.enter_context(tc.tile_pool(name="single_pool", bufs=8))
         double_pool = ctx.enter_context(tc.tile_pool(name="double_pool", bufs=8))
@@ -85,7 +85,7 @@ def tile_attention_pa_kernel(tc, x, freqs_cos, freqs_sin, wq, wk, out_0, out_1):
         products = {}
 
         def load_x(m):
-            tile = x_pool.tile([P, K], BF16, tag="x_tile")
+            tile = shared_pool.tile([P, K], BF16, tag="x_tile_%d" % m, offset=m * K * 2)
             nc.sync.dma_start(out=tile[:], in_=x_rows[m * P : (m + 1) * P, :])
             x_tiles[m] = tile
 
@@ -163,7 +163,9 @@ def tile_attention_pa_kernel(tc, x, freqs_cos, freqs_sin, wq, wk, out_0, out_1):
             taken = [column for routed_g, column in ROUTED.get(c, []) + ROUTED_LATE.get(c, []) if routed_g == g]
             first_column = HALF * len([column for column in taken if column == 0 or len(taken) == 2])
             end_column = min([column for column in taken if column > 0 and len(taken) == 1] + [VECTOR_FROM.get(c, {}).get(g, BLOCK)])
-            if end_column > first_column and g not in GPSIMD_TILES.get(c, []):
+            if (c, g) in GPSIMD_PIECES:
+                end_column = min(end_column, GPSIMD_PIECES[(c, g)][0])
+            if end_column > first_column:
                 interleave(nc.scalar.copy, c, g, first_column, end_column)
 
         def interleave_on_vector(c, g):
@@ -171,9 +173,10 @@ def tile_attention_pa_kernel(tc, x, freqs_cos, freqs_sin, wq, wk, out_0, out_1):
                 interleave(nc.vector.tensor_copy, c, g, VECTOR_FROM[c][g], BLOCK)
 
         def interleave_on_gpsimd(c, g):
+            columns = slice(GPSIMD_PIECES[(c, g)][0], GPSIMD_PIECES[(c, g)][1])
             nc.gpsimd.tensor_scalar(
-                out=w_grouped[(c, g // 2)][:, g % 2, :, :],
-                in0=w_rows[(c, g)].rearrange("p j n -> p n j"),
+                out=w_grouped[(c, g // 2)][:, g % 2, columns, :],
+                in0=w_rows[(c, g)][:, :, columns].rearrange("p j n -> p n j"),
                 scalar1=1.0,
                 scalar2=0.0,
                 op0=MULT,
@@ -293,6 +296,7 @@ def tile_attention_pa_kernel(tc, x, freqs_cos, freqs_sin, wq, wk, out_0, out_1):
             if c == 0:
                 for g in [0, 1]:
                     interleave_on_vector(1, g)
+                interleave_on_gpsimd(1, 1)
             if 0 < c < BLOCKS:
                 quantize_weights(c, 0)
                 quantize_weights(c, 1)
@@ -317,7 +321,10 @@ def tile_attention_pa_kernel(tc, x, freqs_cos, freqs_sin, wq, wk, out_0, out_1):
                 banks.extend([(c - 1, 2), (c - 1, 3)])
             if c < BLOCKS:
                 banks.extend([(c, 0), (c, 1)])
-            tile = products_pool.tile([P, 4, 2, BLOCK], F32, tag="products")
+            if c % 4 == 3:
+                tile = shared_pool.tile([P, 4, 2, BLOCK], F32, tag="products_on_x", offset=0)
+            else:
+                tile = products_pool.tile([P, 4, 2, BLOCK], F32, tag="products")
             for slot, bank in enumerate(banks):
                 multiply_by_factors(*bank, tile, slot)
                 if slot == 0 and on_gpsimd > 0:
@@ -330,6 +337,8 @@ def tile_attention_pa_kernel(tc, x, freqs_cos, freqs_sin, wq, wk, out_0, out_1):
                         add(nc.gpsimd, previous_tile, first, first + on_gpsimd)
                         for s in range(first, first + on_gpsimd):
                             store(*previous[s], previous_tile[:, s, 0, :])
+                        if c == 1:
+                            interleave_on_gpsimd(2, 0)
             if c == BLOCKS and on_vector > 0:
                 add(nc.vector, previous_tile, on_gpsimd, len(previous))
                 for s in range(on_gpsimd, len(previous)):

from contextlib import ExitStack

import concourse.mybir as mybir
from concourse.masks import make_identity

F32 = mybir.dt.float32
BF16 = mybir.dt.bfloat16
U32 = mybir.dt.uint32
U8 = mybir.dt.uint8
E5M2_X4 = mybir.dt.float8_e5m2_x4
MULT = mybir.AluOpType.mult
ADD = mybir.AluOpType.add

P = 128
TOKENS = 512
K = 2048
FEATURES = 2048
HEAD_DIM = 128
PAIRS = HEAD_DIM // 2
PACK = 4
K_PASS = P * PACK
PASSES = K // K_PASS
TOKEN_TILES = TOKENS // P
BLOCK = 512
BLOCKS_PER_MATRIX = FEATURES // BLOCK
BLOCKS = 2 * BLOCKS_PER_MATRIX
HEADS_PER_BLOCK = BLOCK // HEAD_DIM
RUN = 4
HALF = BLOCK // 2

FLOPS = 2 * TOKENS * K * 2 * FEATURES

VECTOR_FROM = {0: {0: 192, 1: 192, 2: 192, 3: 192}, 1: {1: 248, 3: 256}, 2: {3: 0}}
ROUTED = {3: [(0, 0), (0, 256)], 4: [(0, 0), (0, 256)], 5: [(0, 0), (0, 256)], 6: [(0, 0), (0, 256)], 7: [(0, 0), (0, 256)]}
ROUTED_LATE = {7: [(3, 0), (3, 256)]}
GPSIMD_PIECES = {(1, 1): (0, 256), (2, 0): (352, 512)}
GPSIMD_ADDS = 3
PAIRED = [1,2,3]
X_ON_VECTOR = []


def tile_attention_pa_kernel(tc, x, freqs_cos, freqs_sin, wq, wk, out_0, out_1):
    nc = tc.nc
    x_rows = x.rearrange("b s k -> (b s) k")
    out_rows = [out_0.rearrange("b s h d -> (b s) (h d)"), out_1.rearrange("b s h d -> (b s) (h d)")]
    weights = [wq, wk]

    with ExitStack() as ctx:
        const = ctx.enter_context(tc.tile_pool(name="const", bufs=1))
        shared_pool = ctx.enter_context(tc.tile_pool(name="shared_pool", bufs=1))
        x_grouped_pool = ctx.enter_context(tc.tile_pool(name="x_grouped_pool", bufs=2))
        single_pool = ctx.enter_context(tc.tile_pool(name="single_pool", bufs=8))
        double_pool = ctx.enter_context(tc.tile_pool(name="double_pool", bufs=8))
        grouped_pool = ctx.enter_context(tc.tile_pool(name="grouped_pool", bufs=4))
        codes_pool = ctx.enter_context(tc.tile_pool(name="codes_pool", bufs=2))
        products_pool = ctx.enter_context(tc.tile_pool(name="products_pool", bufs=3))
        sums_pool = ctx.enter_context(tc.psum_pool(name="sums_pool", bufs=5))
        routed_pool = ctx.enter_context(tc.psum_pool(name="routed_pool", bufs=3))
        ctx.enter_context(tc.manual_schedule())

        identity = const.tile([P, P], F32)
        make_identity(nc, identity[:])
        identity_bf16 = const.tile([P, P], BF16)
        make_identity(nc, identity_bf16[:])
        warm_in = const.tile([P, 8], F32)
        warm_out = const.tile([P, 8], F32)
        nc.vector.memset(warm_in[:], 0.0)
        nc.scalar.copy(out=warm_out[:], in_=warm_in[:])

        cos_bf16 = const.tile([P, TOKEN_TILES, PAIRS], BF16)
        sin_bf16 = const.tile([P, TOKEN_TILES, PAIRS], BF16)
        factors = const.tile([P, TOKEN_TILES, 2, HEAD_DIM], F32)
        x_codes = const.tile([P, TOKEN_TILES, K_PASS], U32, align_bytes=64)
        x_scales = const.tile([P, TOKEN_TILES, K_PASS], U8, align_bytes=64)

        x_tiles = {}
        x_turned = {}
        x_grouped = {}
        w_rows = {}
        w_grouped = {}
        w_codes = {}
        w_scales = {}
        routed = {}
        sums = {}
        products = {}

        def load_x(m):
            tile = shared_pool.tile([P, K], BF16, tag="x_tile_%d" % m, offset=m * K * 2)
            nc.sync.dma_start(out=tile[:], in_=x_rows[m * P : (m + 1) * P, :])
            x_tiles[m] = tile

        def load_factors():
            nc.scalar.dma_start(out=cos_bf16[:], in_=freqs_cos.rearrange("(m p) i -> p m i", p=P))
            nc.scalar.dma_start(out=sin_bf16[:], in_=freqs_sin.rearrange("(m p) i -> p m i", p=P))

        def k_rows(matrix, g, first_column, columns):
            rows = weights[matrix][g * K_PASS : (g + 1) * K_PASS, first_column : first_column + columns]
            return rows.rearrange("(p j) n -> p j n", j=PACK)

        def load_one_block(c, g):
            tile = single_pool.tile([P, PACK, BLOCK], BF16, tag="single")
            matrix, block = divmod(c, BLOCKS_PER_MATRIX)
            nc.sync.dma_start(out=tile[:], in_=k_rows(matrix, g, block * BLOCK, BLOCK))
            w_rows[(c, g)] = tile[:]

        def load_two_blocks(pair, g):
            tile = double_pool.tile([P, PACK, 2 * BLOCK], BF16, tag="double")
            matrix, half_matrix = divmod(pair, BLOCKS_PER_MATRIX // 2)
            nc.sync.dma_start(out=tile[:], in_=k_rows(matrix, g, half_matrix * 2 * BLOCK, 2 * BLOCK))
            w_rows[(2 * pair, g)] = tile[:, :, 0:BLOCK]
            w_rows[(2 * pair + 1, g)] = tile[:, :, BLOCK : 2 * BLOCK]

        def transpose_x(m):
            words = x_tiles[m][:].bitcast(F32)
            for half in range(2):
                if 2 * m + half < 5:
                    bank = sums_pool.tile([P, 4, P], F32, tag="sums")
                else:
                    bank = routed_pool.tile([P, 4, P], F32, tag="routed")
                for g_in_half in range(2):
                    g = 2 * half + g_in_half
                    for u in range(2):
                        nc.tensor.transpose(
                            bank[:, 2 * g_in_half + u, :], words[:, 256 * g + u : 256 * (g + 1) : 2], identity[:]
                        )
                x_turned[(m, half)] = bank

        def copy_x_out(m):
            tile = x_grouped_pool.tile([P, K], BF16, tag="x_grouped", align_bytes=64)
            words = tile[:].bitcast(F32).rearrange("p (g r u) -> p g r u", g=PASSES, u=2)
            for half in range(2):
                copy = nc.vector.tensor_copy if (m, half) in X_ON_VECTOR else nc.scalar.copy
                copy(
                    out=words[:, 2 * half : 2 * half + 2, :, :],
                    in_=x_turned[(m, half)][:].rearrange("p (g u) r -> p g r u", u=2),
                )
            x_grouped[m] = tile

        def quantize_x(m):
            nc.vector.quantize_mx(out=x_codes[:, m, :].bitcast(E5M2_X4), scales=x_scales[:, m, :], in_=x_grouped[m][:])

        def widen_factors():
            by_pair = factors[:].rearrange("p m r (i e) -> p m r i e", e=2)
            nc.scalar.copy(
                out=by_pair[:, :, 0, :, :], in_=cos_bf16[:].unsqueeze(3).to_broadcast([P, TOKEN_TILES, PAIRS, 2])
            )
            nc.scalar.copy(out=by_pair[:, :, 1, :, 0], in_=sin_bf16[:])
            nc.scalar.mul(out=by_pair[:, :, 1, :, 1], in_=sin_bf16[:], mul=-1.0)

        def new_grouped(c):
            for half in range(2):
                tile = grouped_pool.tile([P, 2, BLOCK, PACK], BF16, tag="grouped", align_bytes=64)
                w_grouped[(c, half)] = tile

        def interleave(copy, c, g, first_column, end_column):
            columns = slice(first_column, end_column)
            copy(
                out=w_grouped[(c, g // 2)][:, g % 2, columns, :].rearrange("p (n i) j -> p n j i", i=RUN),
                in_=w_rows[(c, g)][:, :, columns].rearrange("p j (n i) -> p n j i", i=RUN),
            )

        def interleave_on_scalar(c, g):
            taken = [column for routed_g, column in ROUTED.get(c, []) + ROUTED_LATE.get(c, []) if routed_g == g]
            first_column = HALF * len([column for column in taken if column == 0 or len(taken) == 2])
            end_column = min([column for column in taken if column > 0 and len(taken) == 1] + [VECTOR_FROM.get(c, {}).get(g, BLOCK)])
            if (c, g) in GPSIMD_PIECES:
                end_column = min(end_column, GPSIMD_PIECES[(c, g)][0])
            if end_column > first_column:
                interleave(nc.scalar.copy, c, g, first_column, end_column)

        def interleave_on_vector(c, g):
            if g in VECTOR_FROM.get(c, {}):
                interleave(nc.vector.tensor_copy, c, g, VECTOR_FROM[c][g], BLOCK)

        def interleave_on_gpsimd(c, g):
            columns = slice(GPSIMD_PIECES[(c, g)][0], GPSIMD_PIECES[(c, g)][1])
            nc.gpsimd.tensor_scalar(
                out=w_grouped[(c, g // 2)][:, g % 2, columns, :],
                in0=w_rows[(c, g)][:, :, columns].rearrange("p j n -> p n j"),
                scalar1=1.0,
                scalar2=0.0,
                op0=MULT,
                op1=ADD,
            )

        def interleave_on_tensor(c, plan):
            for g, first_column in plan.get(c, []):
                bank = routed_pool.tile([P, 2, P, PACK], BF16, tag="routed")
                for r in range(2):
                    columns = slice(first_column + r * P, first_column + (r + 1) * P)
                    nc.tensor.matmul(
                        out=bank[:, r, :, :],
                        lhsT=identity_bf16[:],
                        rhs=w_rows[(c, g)][:, :, columns].rearrange("p j n -> p n j"),
                        start=True,
                        stop=True,
                    )
                routed[(c, g, first_column)] = bank

        def copy_routed_out(c, plan):
            for g, first_column in plan.get(c, []):
                nc.scalar.copy(
                    out=w_grouped[(c, g // 2)][:, g % 2, first_column : first_column + HALF, :].rearrange("p n j -> p (n j)"),
                    in_=routed[(c, g, first_column)][:].rearrange("p r n j -> p (r n j)"),
                )

        def quantize_weights(c, half):
            if half == 0:
                codes = codes_pool.tile([P, PASSES, BLOCK], U32, tag="codes", align_bytes=64)
                scales = codes_pool.tile([P, PASSES, BLOCK], U8, tag="scales", align_bytes=64)
                w_codes[c] = codes
                w_scales[c] = scales
            two_passes = slice(2 * half, 2 * half + 2)
            nc.vector.quantize_mx(
                out=w_codes[c][:, two_passes, :].rearrange("p g n -> p (g n)").bitcast(E5M2_X4),
                scales=w_scales[c][:, two_passes, :].rearrange("p g n -> p (g n)"),
                in_=w_grouped[(c, half)][:].rearrange("p g n j -> p (g n j)"),
            )

        def multiply(c, m, passes):
            if passes[0] == 0:
                bank = sums_pool.tile([P, BLOCK], F32, tag="sums")
                sums[(c, m)] = bank
            for g in passes:
                tokens = slice(g * P, (g + 1) * P)
                nc.tensor.matmul_mx(
                    out=sums[(c, m)][:],
                    lhsT=x_codes[:, m, tokens].bitcast(E5M2_X4),
                    lhsT_scale=x_scales[:, m, tokens],
                    rhs=w_codes[c][:, g, :].bitcast(E5M2_X4),
                    rhs_scale=w_scales[c][:, g, :],
                    start=(g == 0),
                    stop=(g == PASSES - 1),
                )

        def multiply_by_factors(c, m, tile, slot):
            shape = [P, 2, HEADS_PER_BLOCK, HEAD_DIM]
            nc.vector.tensor_tensor(
                out=tile[:, slot, :, :].rearrange("p r (h d) -> p r h d", h=HEADS_PER_BLOCK),
                in0=sums[(c, m)][:].rearrange("p (h d) -> p h d", h=HEADS_PER_BLOCK).unsqueeze(1).to_broadcast(shape),
                in1=factors[:, m, :, :].unsqueeze(2).to_broadcast(shape),
                op=MULT,
            )

        def add(engine, tile, first, end, result=None):
            if result is None:
                result = tile[:, first:end, 0, :]
            engine.tensor_tensor(
                out=result.rearrange("p b (n e) -> p b n e", e=2),
                in0=tile[:, first:end, 0, :].rearrange("p b (n e) -> p b n e", e=2),
                in1=tile[:, first:end, 1, :].rearrange("p b (n e) -> p b n e", e=2)[:, :, :, ::-1],
                op=ADD,
            )

        def store(c, m, result):
            matrix, block = divmod(c, BLOCKS_PER_MATRIX)
            nc.sync.dma_start(out=out_rows[matrix][m * P : (m + 1) * P, block * BLOCK : (block + 1) * BLOCK], in_=result)

        load_factors()
        for m in range(TOKEN_TILES):
            load_x(m)
            load_one_block(0, m)
        for g in range(PASSES):
            load_one_block(1, g)
        for pair in [1, 2]:
            for g in range(PASSES):
                load_two_blocks(pair, g)

        widen_factors()
        for m in range(TOKEN_TILES):
            transpose_x(m)
        new_grouped(0)
        for m in range(TOKEN_TILES):
            copy_x_out(m)
            interleave_on_scalar(0, m)
            interleave_on_vector(0, m)
            quantize_x(m)
            if m == 1:
                quantize_weights(0, 0)
        quantize_weights(0, 1)
        for m in range(TOKEN_TILES):
            multiply(0, m, [0, 1])
        for m in range(TOKEN_TILES):
            multiply(0, m, [2, 3])

        all_passes = list(range(PASSES))
        previous = []
        previous_tile = None
        for c in range(BLOCKS + 1):
            following = c + 1
            if following < BLOCKS:
                new_grouped(following)
                copy_routed_out(following, ROUTED)
                for g in range(PASSES):
                    interleave_on_scalar(following, g)
            if c == 0:
                for g in [0, 1]:
                    interleave_on_vector(1, g)
                interleave_on_gpsimd(1, 1)
            if 0 < c < BLOCKS:
                quantize_weights(c, 0)
                quantize_weights(c, 1)
                multiply(c, 0, all_passes)
                multiply(c, 1, all_passes)
            interleave_on_tensor(c + 2, ROUTED)
            interleave_on_tensor(c + 1, ROUTED_LATE)
            copy_routed_out(c + 1, ROUTED_LATE)
            if 0 < c < BLOCKS:
                multiply(c, 2, all_passes)
                multiply(c, 3, all_passes)
            on_gpsimd = min(3, len(previous)) if c < BLOCKS else 2
            on_vector = len(previous) - on_gpsimd
            if c < BLOCKS:
                for slot in range(on_vector):
                    add(nc.vector, previous_tile, slot, slot + 1)
                    store(*previous[slot], previous_tile[:, slot, 0, :])
                if on_vector == 0 and on_gpsimd > 0:
                    nc.vector.tensor_copy(out=previous_tile[:, 0, 1, 0:2], in_=previous_tile[:, 0, 1, 0:2])
            banks = []
            if c > 0:
                banks.extend([(c - 1, 2), (c - 1, 3)])
            if c < BLOCKS:
                banks.extend([(c, 0), (c, 1)])
            if c % 4 == 3:
                tile = shared_pool.tile([P, 4, 2, BLOCK], F32, tag="products_on_x", offset=0)
            else:
                tile = products_pool.tile([P, 4, 2, BLOCK], F32, tag="products")
            for slot, bank in enumerate(banks):
                multiply_by_factors(*bank, tile, slot)
                if slot == 0 and on_gpsimd > 0:
                    first = on_vector if c < BLOCKS else 0
                    if c < BLOCKS and on_vector > 0:
                        add(nc.gpsimd, previous_tile, first, first + on_gpsimd, previous_tile[:, first - 1 : first + on_gpsimd - 1, 1, :])
                        for s in range(first, first + on_gpsimd):
                            store(*previous[s], previous_tile[:, s - 1, 1, :])
                    else:
                        add(nc.gpsimd, previous_tile, first, first + on_gpsimd)
                        for s in range(first, first + on_gpsimd):
                            store(*previous[s], previous_tile[:, s, 0, :])
                        if c == 1:
                            interleave_on_gpsimd(2, 0)
            if c == BLOCKS and on_vector > 0:
                add(nc.vector, previous_tile, on_gpsimd, len(previous))
                for s in range(on_gpsimd, len(previous)):
                    store(*previous[s], previous_tile[:, s, 0, :])
            if following < BLOCKS:
                for g in range(PASSES):
                    if not (c == 0 and g in [0, 1]):
                        interleave_on_vector(following, g)
            for late_pair in {2: [3]}.get(c, []):
                for g in range(PASSES):
                    load_two_blocks(late_pair, g)
            previous = banks
            previous_tile = tile
        for slot in range(len(previous)):
            add(nc.vector, previous_tile, slot, slot + 1)
            store(*previous[slot], previous_tile[:, slot, 0, :])
